import numpy as np
import ml_dtypes

BF16 = ml_dtypes.bfloat16


def bf(x):
    return np.asarray(x, np.float32).astype(BF16)


def f32(x):
    return np.asarray(x, np.float32)


def f64(x):
    return np.asarray(x).astype(np.float64)


def striped(idx):
    return np.tile(idx.reshape(-1, 16).T, (8, 1))


C, S, N, K, H = 768, 256, 1024, 8, 128
EPS = 1e-5


def setup_inputs():
    return {"tok_emb": f32(np.random.standard_normal((C, S))), "pos_emb": f32(np.random.standard_normal((C, N))), "ln_w": f32(1.0 + 0.1 * np.random.standard_normal((C, 1))), "ln_b": f32(0.1 * np.random.standard_normal((C, 1))), "offs": striped(np.concatenate([np.random.permutation(S)[:H] for _ in range(K)]))}


def reference(tok_emb, pos_emb, ln_w, ln_b, offs):
    idx = offs[:16].T.reshape(-1)
    x = f64(tok_emb)[:, idx] + f64(pos_emb)
    mu = x.mean(axis=0, keepdims=True)
    xc = x - mu
    var = (xc * xc).mean(axis=0, keepdims=True)
    h = xc / np.sqrt(var + EPS) * f64(ln_w) + f64(ln_b)
    return np.concatenate([x, h], axis=0)

@@ -1,0 +1,131 @@
+from contextlib import ExitStack
+
+import concourse.mybir as mybir
+from concourse.masks import make_identity
+
+F32 = mybir.dt.float32
+U16 = mybir.dt.uint16
+ADD = mybir.AluOpType.add
+MULT = mybir.AluOpType.mult
+POW = mybir.AluOpType.pow
+IDENTITY = mybir.ActivationFunctionType.Identity
+
+P = 128
+C = 768
+CB = C // P
+V = 256
+N = 1024
+PIECE = 256
+PIECES = N // PIECE
+JB = PIECE // P
+HALF_CB = CB // 2
+HALF_C = C // 2
+BANK = 512
+STATS = 6
+EPS = 1e-5
+
+
+def tile_consciouslm_kernel(tc, tok_emb, pos_emb, ln_w, ln_b, offs, out):
+    nc = tc.nc
+    pos_blocks = pos_emb.rearrange("(b p) j -> p b j", p=P)
+    x_out = out[0:C, :].rearrange("(b p) j -> p b j", p=P)
+    h_out = out[C : 2 * C, :].rearrange("(b p) j -> p b j", p=P)
+
+    with ExitStack() as ctx:
+        held = ctx.enter_context(tc.tile_pool(name="held", bufs=1))
+        pos_pool = ctx.enter_context(tc.tile_pool(name="pos_pool", bufs=PIECES))
+        x_pool = ctx.enter_context(tc.tile_pool(name="x_pool", bufs=PIECES))
+        h_pool = ctx.enter_context(tc.tile_pool(name="h_pool", bufs=PIECES))
+        xn_pool = ctx.enter_context(tc.tile_pool(name="xn_pool", bufs=4))
+        small = ctx.enter_context(tc.tile_pool(name="small", bufs=4))
+        setup_psum = ctx.enter_context(tc.psum_pool(name="setup_psum", bufs=1))
+        xt_psum = ctx.enter_context(tc.psum_pool(name="xt_psum", bufs=2))
+        h_psum = ctx.enter_context(tc.psum_pool(name="h_psum", bufs=1))
+
+        offsets = held.tile([P, N // 16], U16, name="offsets")
+        nc.sync.dma_start(offsets[:], offs)
+        tok = []
+        pos = []
+        for b in range(CB):
+            tok.append(held.tile([P, V], F32, name=f"tok{b}"))
+        for s in range(PIECES):
+            pos_s = pos_pool.tile([P, CB, PIECE], F32, name="pos_s")
+            pos.append(pos_s)
+        for half in range(2):
+            blocks = slice(half * HALF_CB, (half + 1) * HALF_CB)
+            for b in range(half * HALF_CB, (half + 1) * HALF_CB):
+                nc.sync.dma_start(tok[b][:], tok_emb[b * P : (b + 1) * P, :])
+            nc.sync.dma_start(pos[0][:, blocks, :], pos_blocks[:, blocks, 0:PIECE])
+        for s in range(1, PIECES):
+            for half in range(2):
+                blocks = slice(half * HALF_CB, (half + 1) * HALF_CB)
+                nc.sync.dma_start(pos[s][:, blocks, :], pos_blocks[:, blocks, s * PIECE : (s + 1) * PIECE])
+
+        ident = held.tile([P, P], F32, name="ident")
+        make_identity(nc, ident[:])
+        neg_half = held.tile([P, 1], F32, name="neg_half")
+        nc.gpsimd.memset(neg_half[:], -0.5)
+
+        wb_rows = held.tile([P, P], F32, name="wb_rows")
+        nc.gpsimd.memset(wb_rows[:], 0.0)
+        nc.sync.dma_start(wb_rows[0:CB, :], ln_w.rearrange("(b p) o -> b (p o)", p=P))
+        nc.sync.dma_start(wb_rows[CB : 2 * CB, :], ln_b.rearrange("(b p) o -> b (p o)", p=P))
+        wb_ps = setup_psum.tile([P, P], F32, name="wb_ps")
+        nc.tensor.transpose(wb_ps[:], wb_rows[:], ident[:])
+        wb = held.tile([P, 2 * CB], F32, name="wb")
+        nc.vector.tensor_copy(wb[:], wb_ps[:, 0 : 2 * CB])
+
+        def look_up_and_add(s):
+            x_s = x_pool.tile([P, CB, PIECE], F32, name="x_s")
+            piece_offsets = offsets[:, s * (PIECE // 16) : (s + 1) * (PIECE // 16)]
+            for b in range(CB):
+                nc.vector.tensor_tensor(x_s[:, b, :], tok[b][:].indirect(piece_offsets), pos[s][:, b, :], ADD)
+            nc.sync.dma_start(x_out[:, :, s * PIECE : (s + 1) * PIECE], x_s[:])
+            return x_s
+
+        def layer_norm(s, x_s):
+            h_ps = h_psum.tile([P, CB, PIECE], F32, name="h_ps")
+            for t in range(JB):
+                xt = xt_psum.tile([P, 2, BANK], F32, name="xt")
+                for b in range(CB):
+                    nc.tensor.transpose(
+                        xt[:, b // HALF_CB, (b % HALF_CB) * P : (b % HALF_CB + 1) * P],
+                        x_s[:, b, t * P : (t + 1) * P],
+                        ident[:],
+                    )
+                stats = small.tile([P, 2 * STATS], F32, name="stats")
+                for half in range(2):
+                    nc.vector.bn_stats(stats[:, half * STATS : (half + 1) * STATS], xt[:, half, 0:HALF_C])
+                mean_var = small.tile([P, 2], F32, name="mean_var")
+                nc.vector.bn_aggr(mean_var[:], stats[:])
+                var_eps = small.tile([P, 1], F32, name="var_eps")
+                nc.gpsimd.tensor_scalar(var_eps[:], mean_var[:, 1:2], EPS, 1.0, ADD, MULT)
+                rstd = small.tile([P, 1], F32, name="rstd")
+                nc.gpsimd.tensor_tensor(rstd[:], var_eps[:], neg_half[:], POW)
+                shift = small.tile([P, 1], F32, name="shift")
+                nc.gpsimd.tensor_scalar(shift[:], mean_var[:, 0:1], rstd[:, 0:1], -1.0, MULT, MULT)
+                xn = xn_pool.tile([P, C], F32, name="xn")
+                for half in range(2):
+                    nc.scalar.activation(
+                        xn[:, half * HALF_C : (half + 1) * HALF_C],
+                        xt[:, half, 0:HALF_C],
+                        IDENTITY,
+                        bias=shift[:, 0:1],
+                        scale=rstd[:, 0:1],
+                    )
+                for b in range(CB):
+                    nc.tensor.transpose(h_ps[:, b, t * P : (t + 1) * P], xn[:, b * P : (b + 1) * P], ident[:])
+            h_s = h_pool.tile([P, CB, PIECE], F32, name="h_s")
+            for half in range(2):
+                blocks = slice(half * HALF_CB, (half + 1) * HALF_CB)
+                for b in range(half * HALF_CB, (half + 1) * HALF_CB):
+                    nc.scalar.activation(
+                        h_s[:, b, :], h_ps[:, b, :], IDENTITY, bias=wb[:, CB + b : CB + b + 1], scale=wb[:, b : b + 1]
+                    )
+                nc.sync.dma_start(h_out[:, blocks, s * PIECE : (s + 1) * PIECE], h_s[:, blocks, :])
+
+        x_tiles = [look_up_and_add(0)]
+        for s in range(PIECES):
+            if s + 1 < PIECES:
+                x_tiles.append(look_up_and_add(s + 1))
+            layer_norm(s, x_tiles[s])

@@ -6,15 +6,15 @@ from concourse.masks import make_identity
 F32 = mybir.dt.float32
 U16 = mybir.dt.uint16
 ADD = mybir.AluOpType.add
-MULT = mybir.AluOpType.mult
-POW = mybir.AluOpType.pow
 IDENTITY = mybir.ActivationFunctionType.Identity
+ABS_RSQRT = mybir.ActivationFunctionType.Abs_reciprocal_sqrt
 
 P = 128
 C = 768
 CB = C // P
 V = 256
 N = 1024
+BLOCKS = N // P
 PIECE = 256
 PIECES = N // PIECE
 JB = PIECE // P
@@ -23,6 +23,7 @@ HALF_C = C // 2
 BANK = 512
 STATS = 6
 EPS = 1e-5
+POS_RING = 3
 
 
 def tile_consciouslm_kernel(tc, tok_emb, pos_emb, ln_w, ln_b, offs, out):
@@ -33,99 +34,132 @@ def tile_consciouslm_kernel(tc, tok_emb, pos_emb, ln_w, ln_b, offs, out):
 
     with ExitStack() as ctx:
         held = ctx.enter_context(tc.tile_pool(name="held", bufs=1))
-        pos_pool = ctx.enter_context(tc.tile_pool(name="pos_pool", bufs=PIECES))
+        pos_pool = ctx.enter_context(tc.tile_pool(name="pos_pool", bufs=POS_RING))
         x_pool = ctx.enter_context(tc.tile_pool(name="x_pool", bufs=PIECES))
         h_pool = ctx.enter_context(tc.tile_pool(name="h_pool", bufs=PIECES))
-        xn_pool = ctx.enter_context(tc.tile_pool(name="xn_pool", bufs=4))
+        xn_pool = ctx.enter_context(tc.tile_pool(name="xn_pool", bufs=3))
         small = ctx.enter_context(tc.tile_pool(name="small", bufs=4))
-        setup_psum = ctx.enter_context(tc.psum_pool(name="setup_psum", bufs=1))
-        xt_psum = ctx.enter_context(tc.psum_pool(name="xt_psum", bufs=2))
-        h_psum = ctx.enter_context(tc.psum_pool(name="h_psum", bufs=1))
 
         offsets = held.tile([P, N // 16], U16, name="offsets")
         nc.sync.dma_start(offsets[:], offs)
+
         tok = []
-        pos = []
         for b in range(CB):
             tok.append(held.tile([P, V], F32, name=f"tok{b}"))
-        for s in range(PIECES):
-            pos_s = pos_pool.tile([P, CB, PIECE], F32, name="pos_s")
-            pos.append(pos_s)
-        for half in range(2):
-            blocks = slice(half * HALF_CB, (half + 1) * HALF_CB)
-            for b in range(half * HALF_CB, (half + 1) * HALF_CB):
-                nc.sync.dma_start(tok[b][:], tok_emb[b * P : (b + 1) * P, :])
-            nc.sync.dma_start(pos[0][:, blocks, :], pos_blocks[:, blocks, 0:PIECE])
-        for s in range(1, PIECES):
-            for half in range(2):
-                blocks = slice(half * HALF_CB, (half + 1) * HALF_CB)
-                nc.sync.dma_start(pos[s][:, blocks, :], pos_blocks[:, blocks, s * PIECE : (s + 1) * PIECE])
+
+        pos_tiles = []
+        for k in range(POS_RING):
+            pos_k = pos_pool.tile([P, CB, P], F32, name="pos_k")
+            pos_tiles.append(pos_k)
+
+        wb_rows = held.tile([2 * CB, P], F32, name="wb_rows")
+
+        first_loads = [(tok[0][:], tok_emb[0:P, :]), (pos_tiles[0][:], pos_blocks[:, :, 0:P])]
+        for b in range(1, CB):
+            first_loads.append((tok[b][:], tok_emb[b * P : (b + 1) * P, :]))
+        for k in range(1, POS_RING):
+            first_loads.append((pos_tiles[k][:], pos_blocks[:, :, k * P : (k + 1) * P]))
+        first_loads.append((wb_rows[0:CB, :], ln_w.rearrange("(b p) o -> b (p o)", p=P)))
+        first_loads.append((wb_rows[CB : 2 * CB, :], ln_b.rearrange("(b p) o -> b (p o)", p=P)))
+        for n, (tile_ap, dram_ap) in enumerate(first_loads):
+            queue = nc.scalar if n % 2 == 0 else nc.sync
+            queue.dma_start(tile_ap, dram_ap)
+
+        def load_pos(k):
+            pos_k = pos_pool.tile([P, CB, P], F32, name="pos_k")
+            nc.sync.dma_start(pos_k[:], pos_blocks[:, :, k * P : (k + 1) * P])
+            pos_tiles.append(pos_k)
 
         ident = held.tile([P, P], F32, name="ident")
         make_identity(nc, ident[:])
-        neg_half = held.tile([P, 1], F32, name="neg_half")
-        nc.gpsimd.memset(neg_half[:], -0.5)
+        eps = held.tile([P, 1], F32, name="eps")
+        nc.gpsimd.memset(eps[:], EPS)
 
-        wb_rows = held.tile([P, P], F32, name="wb_rows")
-        nc.gpsimd.memset(wb_rows[:], 0.0)
-        nc.sync.dma_start(wb_rows[0:CB, :], ln_w.rearrange("(b p) o -> b (p o)", p=P))
-        nc.sync.dma_start(wb_rows[CB : 2 * CB, :], ln_b.rearrange("(b p) o -> b (p o)", p=P))
-        wb_ps = setup_psum.tile([P, P], F32, name="wb_ps")
-        nc.tensor.transpose(wb_ps[:], wb_rows[:], ident[:])
+        xt_psum = ctx.enter_context(tc.psum_pool(name="xt_psum", bufs=3))
+        h_psum = ctx.enter_context(tc.psum_pool(name="h_psum", bufs=2))
+
+        wb_ps = h_psum.tile([P, BANK], F32, name="h_ps")
+        nc.tensor.matmul(wb_ps[:, 0 : 2 * CB], wb_rows[:], ident[0 : 2 * CB, 0 : 2 * CB], start=True, stop=True)
         wb = held.tile([P, 2 * CB], F32, name="wb")
-        nc.vector.tensor_copy(wb[:], wb_ps[:, 0 : 2 * CB])
+        nc.scalar.copy(wb[:], wb_ps[:, 0 : 2 * CB])
 
-        def look_up_and_add(s):
-            x_s = x_pool.tile([P, CB, PIECE], F32, name="x_s")
-            piece_offsets = offsets[:, s * (PIECE // 16) : (s + 1) * (PIECE // 16)]
+        x_tiles = []
+        h_tiles = []
+        xt_tiles = []
+        scales = []
+
+        def look_up_add_and_turn(k):
+            s, t = divmod(k, JB)
+            if t == 0:
+                x_new = x_pool.tile([P, CB, PIECE], F32, name="x_new")
+                x_tiles.append(x_new)
+            x_s = x_tiles[s]
+            block_offsets = offsets[:, k * (P // 16) : (k + 1) * (P // 16)]
+            xt = xt_psum.tile([P, 2, BANK], F32, name="xt")
+            xt_tiles.append(xt)
             for b in range(CB):
-                nc.vector.tensor_tensor(x_s[:, b, :], tok[b][:].indirect(piece_offsets), pos[s][:, b, :], ADD)
-            nc.sync.dma_start(x_out[:, :, s * PIECE : (s + 1) * PIECE], x_s[:])
-            return x_s
+                x_block = x_s[:, b, t * P : (t + 1) * P]
+                nc.vector.tensor_tensor(x_block, tok[b][:].indirect(block_offsets), pos_tiles[k][:, b, :], ADD)
+                nc.tensor.transpose(xt[:, b // HALF_CB, (b % HALF_CB) * P : (b % HALF_CB + 1) * P], x_block, ident[:])
+            if t == JB - 1:
+                nc.sync.dma_start(x_out[:, :, s * PIECE : (s + 1) * PIECE], x_s[:])
 
-        def layer_norm(s, x_s):
-            h_ps = h_psum.tile([P, CB, PIECE], F32, name="h_ps")
-            for t in range(JB):
-                xt = xt_psum.tile([P, 2, BANK], F32, name="xt")
-                for b in range(CB):
-                    nc.tensor.transpose(
-                        xt[:, b // HALF_CB, (b % HALF_CB) * P : (b % HALF_CB + 1) * P],
-                        x_s[:, b, t * P : (t + 1) * P],
-                        ident[:],
-                    )
-                stats = small.tile([P, 2 * STATS], F32, name="stats")
-                for half in range(2):
-                    nc.vector.bn_stats(stats[:, half * STATS : (half + 1) * STATS], xt[:, half, 0:HALF_C])
-                mean_var = small.tile([P, 2], F32, name="mean_var")
-                nc.vector.bn_aggr(mean_var[:], stats[:])
-                var_eps = small.tile([P, 1], F32, name="var_eps")
-                nc.gpsimd.tensor_scalar(var_eps[:], mean_var[:, 1:2], EPS, 1.0, ADD, MULT)
-                rstd = small.tile([P, 1], F32, name="rstd")
-                nc.gpsimd.tensor_tensor(rstd[:], var_eps[:], neg_half[:], POW)
-                shift = small.tile([P, 1], F32, name="shift")
-                nc.gpsimd.tensor_scalar(shift[:], mean_var[:, 0:1], rstd[:, 0:1], -1.0, MULT, MULT)
-                xn = xn_pool.tile([P, C], F32, name="xn")
-                for half in range(2):
-                    nc.scalar.activation(
-                        xn[:, half * HALF_C : (half + 1) * HALF_C],
-                        xt[:, half, 0:HALF_C],
-                        IDENTITY,
-                        bias=shift[:, 0:1],
-                        scale=rstd[:, 0:1],
-                    )
-                for b in range(CB):
-                    nc.tensor.transpose(h_ps[:, b, t * P : (t + 1) * P], xn[:, b * P : (b + 1) * P], ident[:])
-            h_s = h_pool.tile([P, CB, PIECE], F32, name="h_s")
+        def statistics(k):
+            xt = xt_tiles[k]
+            stats = small.tile([P, 2 * STATS], F32, name="stats")
             for half in range(2):
-                blocks = slice(half * HALF_CB, (half + 1) * HALF_CB)
-                for b in range(half * HALF_CB, (half + 1) * HALF_CB):
-                    nc.scalar.activation(
-                        h_s[:, b, :], h_ps[:, b, :], IDENTITY, bias=wb[:, CB + b : CB + b + 1], scale=wb[:, b : b + 1]
-                    )
-                nc.sync.dma_start(h_out[:, blocks, s * PIECE : (s + 1) * PIECE], h_s[:, blocks, :])
+                nc.vector.bn_stats(stats[:, half * STATS : (half + 1) * STATS], xt[:, half, 0:HALF_C])
+            mean_var = small.tile([P, 2], F32, name="mean_var")
+            nc.vector.bn_aggr(mean_var[:], stats[:])
+            rstd = small.tile([P, 1], F32, name="rstd")
+            nc.scalar.activation(rstd[:], mean_var[:, 1:2], ABS_RSQRT, bias=eps[:, 0:1])
+            neg_mean = small.tile([P, 1], F32, name="neg_mean")
+            nc.scalar.mul(neg_mean[:], mean_var[:, 0:1], -1.0)
+            shift = small.tile([P, 1], F32, name="shift")
+            nc.scalar.activation(shift[:], neg_mean[:], IDENTITY, scale=rstd[:, 0:1])
+            scales.append((rstd, shift))
 
-        x_tiles = [look_up_and_add(0)]
-        for s in range(PIECES):
-            if s + 1 < PIECES:
-                x_tiles.append(look_up_and_add(s + 1))
-            layer_norm(s, x_tiles[s])
+        def normalise_turn_back_gain_bias(k):
+            s, t = divmod(k, JB)
+            xt = xt_tiles[k]
+            rstd, shift = scales[k]
+            if t == 0:
+                h_new = h_pool.tile([P, CB, PIECE], F32, name="h_new")
+                h_tiles.append(h_new)
+            h_s = h_tiles[s]
+            xn = xn_pool.tile([P, C], F32, name="xn")
+            for half in range(2):
+                nc.scalar.activation(
+                    xn[:, half * HALF_C : (half + 1) * HALF_C],
+                    xt[:, half, 0:HALF_C],
+                    IDENTITY,
+                    bias=shift[:, 0:1],
+                    scale=rstd[:, 0:1],
+                )
+            for half in range(2):
+                h_ps = h_psum.tile([P, BANK], F32, name="h_ps")
+                for i in range(HALF_CB):
+                    b = half * HALF_CB + i
+                    nc.tensor.transpose(h_ps[:, i * P : (i + 1) * P], xn[:, b * P : (b + 1) * P], ident[:])
+                for i in range(HALF_CB):
+                    b = half * HALF_CB + i
+                    nc.scalar.activation(
+                        h_s[:, b, t * P : (t + 1) * P],
+                        h_ps[:, i * P : (i + 1) * P],
+                        IDENTITY,
+                        bias=wb[:, CB + b : CB + b + 1],
+                        scale=wb[:, b : b + 1],
+                    )
+                if t == JB - 1:
+                    blocks = slice(half * HALF_CB, (half + 1) * HALF_CB)
+                    nc.sync.dma_start(h_out[:, blocks, s * PIECE : (s + 1) * PIECE], h_s[:, blocks, :])
+
+        for i in range(BLOCKS + 2):
+            if i < BLOCKS:
+                look_up_add_and_turn(i)
+            if i + POS_RING < BLOCKS:
+                load_pos(i + POS_RING)
+            if 1 <= i <= BLOCKS:
+                statistics(i - 1)
+            if i >= 2:
+                normalise_turn_back_gain_bias(i - 2)

@@ -12,18 +12,21 @@ ABS_RSQRT = mybir.ActivationFunctionType.Abs_reciprocal_sqrt
 P = 128
 C = 768
 CB = C // P
+HALF_CB = CB // 2
 V = 256
 N = 1024
-BLOCKS = N // P
 PIECE = 256
 PIECES = N // PIECE
 JB = PIECE // P
-HALF_CB = CB // 2
-HALF_C = C // 2
 BANK = 512
 STATS = 6
 EPS = 1e-5
-POS_RING = 3
+POS_RING = 2
+
+
+def bank_chunks(first, last):
+    cuts = [first] + [c for c in range(0, last, BANK) if first < c] + [last]
+    return list(zip(cuts[:-1], cuts[1:]))
 
 
 def tile_consciouslm_kernel(tc, tok_emb, pos_emb, ln_w, ln_b, offs, out):
@@ -31,14 +34,17 @@ def tile_consciouslm_kernel(tc, tok_emb, pos_emb, ln_w, ln_b, offs, out):
     pos_blocks = pos_emb.rearrange("(b p) j -> p b j", p=P)
     x_out = out[0:C, :].rearrange("(b p) j -> p b j", p=P)
     h_out = out[C : 2 * C, :].rearrange("(b p) j -> p b j", p=P)
+    halves = (slice(0, HALF_CB), slice(HALF_CB, CB))
 
     with ExitStack() as ctx:
         held = ctx.enter_context(tc.tile_pool(name="held", bufs=1))
         pos_pool = ctx.enter_context(tc.tile_pool(name="pos_pool", bufs=POS_RING))
         x_pool = ctx.enter_context(tc.tile_pool(name="x_pool", bufs=PIECES))
         h_pool = ctx.enter_context(tc.tile_pool(name="h_pool", bufs=PIECES))
-        xn_pool = ctx.enter_context(tc.tile_pool(name="xn_pool", bufs=3))
+        xn_pool = ctx.enter_context(tc.tile_pool(name="xn_pool", bufs=4))
         small = ctx.enter_context(tc.tile_pool(name="small", bufs=4))
+        xt_psum = ctx.enter_context(tc.psum_pool(name="xt_psum", bufs=2))
+        h_psum = ctx.enter_context(tc.psum_pool(name="h_psum", bufs=2))
 
         offsets = held.tile([P, N // 16], U16, name="offsets")
         nc.sync.dma_start(offsets[:], offs)
@@ -48,35 +54,36 @@ def tile_consciouslm_kernel(tc, tok_emb, pos_emb, ln_w, ln_b, offs, out):
             tok.append(held.tile([P, V], F32, name=f"tok{b}"))
 
         pos_tiles = []
-        for k in range(POS_RING):
-            pos_k = pos_pool.tile([P, CB, P], F32, name="pos_k")
-            pos_tiles.append(pos_k)
+        for s in range(POS_RING):
+            pos_s = pos_pool.tile([P, CB, PIECE], F32, name="pos_s")
+            pos_tiles.append(pos_s)
+
+        def pos_load(s, half):
+            return (pos_tiles[s][:, halves[half], :], pos_blocks[:, halves[half], s * PIECE : (s + 1) * PIECE])
+
+        def tok_load(b):
+            return (tok[b][:], tok_emb[b * P : (b + 1) * P, :])
 
         wb_rows = held.tile([2 * CB, P], F32, name="wb_rows")
 
-        first_loads = [(tok[0][:], tok_emb[0:P, :]), (pos_tiles[0][:], pos_blocks[:, :, 0:P])]
-        for b in range(1, CB):
-            first_loads.append((tok[b][:], tok_emb[b * P : (b + 1) * P, :]))
-        for k in range(1, POS_RING):
-            first_loads.append((pos_tiles[k][:], pos_blocks[:, :, k * P : (k + 1) * P]))
+        first_loads = []
+        for half in range(2):
+            first_loads.append(pos_load(0, half))
+            for b in range(half * HALF_CB, (half + 1) * HALF_CB):
+                first_loads.append(tok_load(b))
         first_loads.append((wb_rows[0:CB, :], ln_w.rearrange("(b p) o -> b (p o)", p=P)))
         first_loads.append((wb_rows[CB : 2 * CB, :], ln_b.rearrange("(b p) o -> b (p o)", p=P)))
+        for s in range(1, POS_RING):
+            for half in range(2):
+                first_loads.append(pos_load(s, half))
         for n, (tile_ap, dram_ap) in enumerate(first_loads):
             queue = nc.scalar if n % 2 == 0 else nc.sync
             queue.dma_start(tile_ap, dram_ap)
-
-        def load_pos(k):
-            pos_k = pos_pool.tile([P, CB, P], F32, name="pos_k")
-            nc.sync.dma_start(pos_k[:], pos_blocks[:, :, k * P : (k + 1) * P])
-            pos_tiles.append(pos_k)
 
         ident = held.tile([P, P], F32, name="ident")
         make_identity(nc, ident[:])
         eps = held.tile([P, 1], F32, name="eps")
         nc.gpsimd.memset(eps[:], EPS)
-
-        xt_psum = ctx.enter_context(tc.psum_pool(name="xt_psum", bufs=3))
-        h_psum = ctx.enter_context(tc.psum_pool(name="h_psum", bufs=2))
 
         wb_ps = h_psum.tile([P, BANK], F32, name="h_ps")
         nc.tensor.matmul(wb_ps[:, 0 : 2 * CB], wb_rows[:], ident[0 : 2 * CB, 0 : 2 * CB], start=True, stop=True)
@@ -84,82 +91,83 @@ def tile_consciouslm_kernel(tc, tok_emb, pos_emb, ln_w, ln_b, offs, out):
         nc.scalar.copy(wb[:], wb_ps[:, 0 : 2 * CB])
 
         x_tiles = []
-        h_tiles = []
         xt_tiles = []
-        scales = []
 
-        def look_up_add_and_turn(k):
-            s, t = divmod(k, JB)
-            if t == 0:
-                x_new = x_pool.tile([P, CB, PIECE], F32, name="x_new")
-                x_tiles.append(x_new)
-            x_s = x_tiles[s]
-            block_offsets = offsets[:, k * (P // 16) : (k + 1) * (P // 16)]
-            xt = xt_psum.tile([P, 2, BANK], F32, name="xt")
+        def look_up_add_and_turn(s):
+            x_s = x_pool.tile([P, CB, PIECE], F32, name="x_s")
+            x_tiles.append(x_s)
+            xt = xt_psum.tile([P, JB * C], F32, name="xt")
             xt_tiles.append(xt)
+            piece_offsets = offsets[:, s * (PIECE // 16) : (s + 1) * (PIECE // 16)]
             for b in range(CB):
-                x_block = x_s[:, b, t * P : (t + 1) * P]
-                nc.vector.tensor_tensor(x_block, tok[b][:].indirect(block_offsets), pos_tiles[k][:, b, :], ADD)
-                nc.tensor.transpose(xt[:, b // HALF_CB, (b % HALF_CB) * P : (b % HALF_CB + 1) * P], x_block, ident[:])
-            if t == JB - 1:
-                nc.sync.dma_start(x_out[:, :, s * PIECE : (s + 1) * PIECE], x_s[:])
-
-        def statistics(k):
-            xt = xt_tiles[k]
-            stats = small.tile([P, 2 * STATS], F32, name="stats")
-            for half in range(2):
-                nc.vector.bn_stats(stats[:, half * STATS : (half + 1) * STATS], xt[:, half, 0:HALF_C])
-            mean_var = small.tile([P, 2], F32, name="mean_var")
-            nc.vector.bn_aggr(mean_var[:], stats[:])
-            rstd = small.tile([P, 1], F32, name="rstd")
-            nc.scalar.activation(rstd[:], mean_var[:, 1:2], ABS_RSQRT, bias=eps[:, 0:1])
-            neg_mean = small.tile([P, 1], F32, name="neg_mean")
-            nc.scalar.mul(neg_mean[:], mean_var[:, 0:1], -1.0)
-            shift = small.tile([P, 1], F32, name="shift")
-            nc.scalar.activation(shift[:], neg_mean[:], IDENTITY, scale=rstd[:, 0:1])
-            scales.append((rstd, shift))
-
-        def normalise_turn_back_gain_bias(k):
-            s, t = divmod(k, JB)
-            xt = xt_tiles[k]
-            rstd, shift = scales[k]
-            if t == 0:
-                h_new = h_pool.tile([P, CB, PIECE], F32, name="h_new")
-                h_tiles.append(h_new)
-            h_s = h_tiles[s]
-            xn = xn_pool.tile([P, C], F32, name="xn")
-            for half in range(2):
-                nc.scalar.activation(
-                    xn[:, half * HALF_C : (half + 1) * HALF_C],
-                    xt[:, half, 0:HALF_C],
-                    IDENTITY,
-                    bias=shift[:, 0:1],
-                    scale=rstd[:, 0:1],
-                )
-            for half in range(2):
-                h_ps = h_psum.tile([P, BANK], F32, name="h_ps")
-                for i in range(HALF_CB):
-                    b = half * HALF_CB + i
-                    nc.tensor.transpose(h_ps[:, i * P : (i + 1) * P], xn[:, b * P : (b + 1) * P], ident[:])
-                for i in range(HALF_CB):
-                    b = half * HALF_CB + i
-                    nc.scalar.activation(
-                        h_s[:, b, t * P : (t + 1) * P],
-                        h_ps[:, i * P : (i + 1) * P],
-                        IDENTITY,
-                        bias=wb[:, CB + b : CB + b + 1],
-                        scale=wb[:, b : b + 1],
+                nc.vector.tensor_tensor(x_s[:, b, :], tok[b][:].indirect(piece_offsets), pos_tiles[s][:, b, :], ADD)
+                for t in range(JB):
+                    nc.tensor.transpose(
+                        xt[:, t * C + b * P : t * C + (b + 1) * P], x_s[:, b, t * P : (t + 1) * P], ident[:]
                     )
-                if t == JB - 1:
-                    blocks = slice(half * HALF_CB, (half + 1) * HALF_CB)
-                    nc.sync.dma_start(h_out[:, blocks, s * PIECE : (s + 1) * PIECE], h_s[:, blocks, :])
+            nc.sync.dma_start(x_out[:, :, s * PIECE : (s + 1) * PIECE], x_s[:])
 
-        for i in range(BLOCKS + 2):
-            if i < BLOCKS:
-                look_up_add_and_turn(i)
-            if i + POS_RING < BLOCKS:
-                load_pos(i + POS_RING)
-            if 1 <= i <= BLOCKS:
-                statistics(i - 1)
-            if i >= 2:
-                normalise_turn_back_gain_bias(i - 2)
+        def load_next_pos(s):
+            pos_s = pos_pool.tile([P, CB, PIECE], F32, name="pos_s")
+            pos_tiles.append(pos_s)
+            for half in range(2):
+                tile_ap, dram_ap = pos_load(s, half)
+                nc.sync.dma_start(tile_ap, dram_ap)
+
+        def layer_norm(s):
+            xt = xt_tiles[s]
+            scales = []
+            for t in range(JB):
+                chunks = bank_chunks(t * C, (t + 1) * C)
+                stats = small.tile([P, len(chunks) * STATS], F32, name="stats")
+                for n, (first, last) in enumerate(chunks):
+                    nc.vector.bn_stats(stats[:, n * STATS : (n + 1) * STATS], xt[:, first:last])
+                mean_var = small.tile([P, 2], F32, name="mean_var")
+                nc.vector.bn_aggr(mean_var[:], stats[:])
+                rstd = small.tile([P, 1], F32, name="rstd")
+                nc.scalar.activation(rstd[:], mean_var[:, 1:2], ABS_RSQRT, bias=eps[:, 0:1])
+                neg_mean = small.tile([P, 1], F32, name="neg_mean")
+                nc.scalar.mul(neg_mean[:], mean_var[:, 0:1], -1.0)
+                shift = small.tile([P, 1], F32, name="shift")
+                nc.scalar.activation(shift[:], neg_mean[:], IDENTITY, scale=rstd[:, 0:1])
+                scales.append((rstd, shift))
+
+            xn_tiles = []
+            for t in range(JB):
+                rstd, shift = scales[t]
+                xn = xn_pool.tile([P, C], F32, name="xn")
+                xn_tiles.append(xn)
+                for first, last in bank_chunks(t * C, (t + 1) * C):
+                    nc.scalar.activation(
+                        xn[:, first - t * C : last - t * C],
+                        xt[:, first:last],
+                        IDENTITY,
+                        bias=shift[:, 0:1],
+                        scale=rstd[:, 0:1],
+                    )
+
+            h_s = h_pool.tile([P, CB, PIECE], F32, name="h_s")
+            for half in range(2):
+                for t in range(JB):
+                    h_ps = h_psum.tile([P, BANK], F32, name="h_ps")
+                    for i in range(HALF_CB):
+                        b = half * HALF_CB + i
+                        nc.tensor.transpose(h_ps[:, i * P : (i + 1) * P], xn_tiles[t][:, b * P : (b + 1) * P], ident[:])
+                    for i in range(HALF_CB):
+                        b = half * HALF_CB + i
+                        nc.scalar.activation(
+                            h_s[:, b, t * P : (t + 1) * P],
+                            h_ps[:, i * P : (i + 1) * P],
+                            IDENTITY,
+                            bias=wb[:, CB + b : CB + b + 1],
+                            scale=wb[:, b : b + 1],
+                        )
+                nc.sync.dma_start(h_out[:, halves[half], s * PIECE : (s + 1) * PIECE], h_s[:, halves[half], :])
+
+        for s in range(PIECES + 1):
+            if s < PIECES:
+                look_up_add_and_turn(s)
+            if s + POS_RING < PIECES:
+                load_next_pos(s + POS_RING)
+            if s >= 1:
+                layer_norm(s - 1)

@@ -105,7 +105,9 @@ def tile_consciouslm_kernel(tc, tok_emb, pos_emb, ln_w, ln_b, offs, out):
                     nc.tensor.transpose(
                         xt[:, t * C + b * P : t * C + (b + 1) * P], x_s[:, b, t * P : (t + 1) * P], ident[:]
                     )
-            nc.sync.dma_start(x_out[:, :, s * PIECE : (s + 1) * PIECE], x_s[:])
+
+        def store_x(s):
+            nc.sync.dma_start(x_out[:, :, s * PIECE : (s + 1) * PIECE], x_tiles[s][:])
 
         def load_next_pos(s):
             pos_s = pos_pool.tile([P, CB, PIECE], F32, name="pos_s")
@@ -169,5 +171,7 @@ def tile_consciouslm_kernel(tc, tok_emb, pos_emb, ln_w, ln_b, offs, out):
                 look_up_add_and_turn(s)
             if s + POS_RING < PIECES:
                 load_next_pos(s + POS_RING)
+            if s < PIECES:
+                store_x(s)
             if s >= 1:
                 layer_norm(s - 1)

@@ -6,6 +6,7 @@ from concourse.masks import make_identity
 F32 = mybir.dt.float32
 U16 = mybir.dt.uint16
 ADD = mybir.AluOpType.add
+MULT = mybir.AluOpType.mult
 IDENTITY = mybir.ActivationFunctionType.Identity
 ABS_RSQRT = mybir.ActivationFunctionType.Abs_reciprocal_sqrt
 
@@ -157,13 +158,23 @@ def tile_consciouslm_kernel(tc, tok_emb, pos_emb, ln_w, ln_b, offs, out):
                         nc.tensor.transpose(h_ps[:, i * P : (i + 1) * P], xn_tiles[t][:, b * P : (b + 1) * P], ident[:])
                     for i in range(HALF_CB):
                         b = half * HALF_CB + i
-                        nc.scalar.activation(
-                            h_s[:, b, t * P : (t + 1) * P],
-                            h_ps[:, i * P : (i + 1) * P],
-                            IDENTITY,
-                            bias=wb[:, CB + b : CB + b + 1],
-                            scale=wb[:, b : b + 1],
-                        )
+                        if half == 0 or s < PIECES - 2:
+                            nc.scalar.activation(
+                                h_s[:, b, t * P : (t + 1) * P],
+                                h_ps[:, i * P : (i + 1) * P],
+                                IDENTITY,
+                                bias=wb[:, CB + b : CB + b + 1],
+                                scale=wb[:, b : b + 1],
+                            )
+                        else:
+                            nc.vector.tensor_scalar(
+                                h_s[:, b, t * P : (t + 1) * P],
+                                h_ps[:, i * P : (i + 1) * P],
+                                wb[:, b : b + 1],
+                                wb[:, CB + b : CB + b + 1],
+                                MULT,
+                                ADD,
+                            )
                 nc.sync.dma_start(h_out[:, halves[half], s * PIECE : (s + 1) * PIECE], h_s[:, halves[half], :])
 
         for s in range(PIECES + 1):

@@ -23,6 +23,7 @@ BANK = 512
 STATS = 6
 EPS = 1e-5
 POS_RING = 2
+X_BYTES = CB * PIECE * 4
 
 
 def bank_chunks(first, last):
@@ -40,7 +41,7 @@ def tile_consciouslm_kernel(tc, tok_emb, pos_emb, ln_w, ln_b, offs, out):
     with ExitStack() as ctx:
         held = ctx.enter_context(tc.tile_pool(name="held", bufs=1))
         pos_pool = ctx.enter_context(tc.tile_pool(name="pos_pool", bufs=POS_RING))
-        x_pool = ctx.enter_context(tc.tile_pool(name="x_pool", bufs=PIECES))
+        x_pool = ctx.enter_context(tc.tile_pool(name="x_pool", bufs=1))
         h_pool = ctx.enter_context(tc.tile_pool(name="h_pool", bufs=PIECES))
         xn_pool = ctx.enter_context(tc.tile_pool(name="xn_pool", bufs=4))
         small = ctx.enter_context(tc.tile_pool(name="small", bufs=4))
@@ -95,7 +96,7 @@ def tile_consciouslm_kernel(tc, tok_emb, pos_emb, ln_w, ln_b, offs, out):
         xt_tiles = []
 
         def look_up_add_and_turn(s):
-            x_s = x_pool.tile([P, CB, PIECE], F32, name="x_s")
+            x_s = x_pool.tile([P, CB, PIECE], F32, name=f"x{s}", offset=s * X_BYTES)
             x_tiles.append(x_s)
             xt = xt_psum.tile([P, JB * C], F32, name="xt")
             xt_tiles.append(xt)
@@ -120,13 +121,12 @@ def tile_consciouslm_kernel(tc, tok_emb, pos_emb, ln_w, ln_b, offs, out):
         def layer_norm(s):
             xt = xt_tiles[s]
             scales = []
+            piece_stats = x_pool.tile([P, JB * 2 * STATS], F32, name=f"stats{s}", offset=(s + 2) * X_BYTES)
             for t in range(JB):
-                chunks = bank_chunks(t * C, (t + 1) * C)
-                stats = small.tile([P, len(chunks) * STATS], F32, name="stats")
-                for n, (first, last) in enumerate(chunks):
-                    nc.vector.bn_stats(stats[:, n * STATS : (n + 1) * STATS], xt[:, first:last])
+                for n, (first, last) in enumerate(bank_chunks(t * C, (t + 1) * C)):
+                    nc.vector.bn_stats(piece_stats[:, (2 * t + n) * STATS : (2 * t + n + 1) * STATS], xt[:, first:last])
                 mean_var = small.tile([P, 2], F32, name="mean_var")
-                nc.vector.bn_aggr(mean_var[:], stats[:])
+                nc.vector.bn_aggr(mean_var[:], piece_stats[:, 2 * t * STATS : 2 * (t + 1) * STATS])
                 rstd = small.tile([P, 1], F32, name="rstd")
                 nc.scalar.activation(rstd[:], mean_var[:, 1:2], ABS_RSQRT, bias=eps[:, 0:1])
                 neg_mean = small.tile([P, 1], F32, name="neg_mean")

@@ -7,6 +7,7 @@ F32 = mybir.dt.float32
 U16 = mybir.dt.uint16
 ADD = mybir.AluOpType.add
 MULT = mybir.AluOpType.mult
+SUBTRACT = mybir.AluOpType.subtract
 IDENTITY = mybir.ActivationFunctionType.Identity
 ABS_RSQRT = mybir.ActivationFunctionType.Abs_reciprocal_sqrt
 
@@ -129,36 +130,52 @@ def tile_consciouslm_kernel(tc, tok_emb, pos_emb, ln_w, ln_b, offs, out):
                 nc.vector.bn_aggr(mean_var[:], piece_stats[:, 2 * t * STATS : 2 * (t + 1) * STATS])
                 rstd = small.tile([P, 1], F32, name="rstd")
                 nc.scalar.activation(rstd[:], mean_var[:, 1:2], ABS_RSQRT, bias=eps[:, 0:1])
-                neg_mean = small.tile([P, 1], F32, name="neg_mean")
-                nc.scalar.mul(neg_mean[:], mean_var[:, 0:1], -1.0)
-                shift = small.tile([P, 1], F32, name="shift")
-                nc.scalar.activation(shift[:], neg_mean[:], IDENTITY, scale=rstd[:, 0:1])
-                scales.append((rstd, shift))
+                if s == PIECES - 1:
+                    scales.append((rstd, mean_var))
+                else:
+                    neg_mean = small.tile([P, 1], F32, name="neg_mean")
+                    nc.scalar.mul(neg_mean[:], mean_var[:, 0:1], -1.0)
+                    shift = small.tile([P, 1], F32, name="shift")
+                    nc.scalar.activation(shift[:], neg_mean[:], IDENTITY, scale=rstd[:, 0:1])
+                    scales.append((rstd, shift))
 
             xn_tiles = []
             for t in range(JB):
-                rstd, shift = scales[t]
+                rstd, shift_or_mean = scales[t]
                 xn = xn_pool.tile([P, C], F32, name="xn")
                 xn_tiles.append(xn)
                 for first, last in bank_chunks(t * C, (t + 1) * C):
-                    nc.scalar.activation(
-                        xn[:, first - t * C : last - t * C],
-                        xt[:, first:last],
-                        IDENTITY,
-                        bias=shift[:, 0:1],
-                        scale=rstd[:, 0:1],
-                    )
+                    if s == PIECES - 1:
+                        nc.vector.tensor_scalar(
+                            xn[:, first - t * C : last - t * C],
+                            xt[:, first:last],
+                            shift_or_mean[:, 0:1],
+                            rstd[:, 0:1],
+                            SUBTRACT,
+                            MULT,
+                        )
+                    else:
+                        nc.scalar.activation(
+                            xn[:, first - t * C : last - t * C],
+                            xt[:, first:last],
+                            IDENTITY,
+                            bias=shift_or_mean[:, 0:1],
+                            scale=rstd[:, 0:1],
+                        )
 
             h_s = h_pool.tile([P, CB, PIECE], F32, name="h_s")
             for half in range(2):
                 for t in range(JB):
-                    h_ps = h_psum.tile([P, BANK], F32, name="h_ps")
+                    if s == PIECES - 1 and half == 0:
+                        h_ps = xt_psum.tile([P, BANK], F32, name="xt")
+                    else:
+                        h_ps = h_psum.tile([P, BANK], F32, name="h_ps")
                     for i in range(HALF_CB):
                         b = half * HALF_CB + i
                         nc.tensor.transpose(h_ps[:, i * P : (i + 1) * P], xn_tiles[t][:, b * P : (b + 1) * P], ident[:])
                     for i in range(HALF_CB):
                         b = half * HALF_CB + i
-                        if half == 0 or s < PIECES - 2:
+                        if half == 0 or s < PIECES - 1:
                             nc.scalar.activation(
                                 h_s[:, b, t * P : (t + 1) * P],
                                 h_ps[:, i * P : (i + 1) * P],

@@ -24,7 +24,6 @@ BANK = 512
 STATS = 6
 EPS = 1e-5
 POS_RING = 2
-X_BYTES = CB * PIECE * 4
 
 
 def bank_chunks(first, last):
@@ -42,7 +41,7 @@ def tile_consciouslm_kernel(tc, tok_emb, pos_emb, ln_w, ln_b, offs, out):
     with ExitStack() as ctx:
         held = ctx.enter_context(tc.tile_pool(name="held", bufs=1))
         pos_pool = ctx.enter_context(tc.tile_pool(name="pos_pool", bufs=POS_RING))
-        x_pool = ctx.enter_context(tc.tile_pool(name="x_pool", bufs=1))
+        x_pool = ctx.enter_context(tc.tile_pool(name="x_pool", bufs=PIECES))
         h_pool = ctx.enter_context(tc.tile_pool(name="h_pool", bufs=PIECES))
         xn_pool = ctx.enter_context(tc.tile_pool(name="xn_pool", bufs=4))
         small = ctx.enter_context(tc.tile_pool(name="small", bufs=4))
@@ -97,7 +96,7 @@ def tile_consciouslm_kernel(tc, tok_emb, pos_emb, ln_w, ln_b, offs, out):
         xt_tiles = []
 
         def look_up_add_and_turn(s):
-            x_s = x_pool.tile([P, CB, PIECE], F32, name=f"x{s}", offset=s * X_BYTES)
+            x_s = x_pool.tile([P, CB, PIECE], F32, name="x_s")
             x_tiles.append(x_s)
             xt = xt_psum.tile([P, JB * C], F32, name="xt")
             xt_tiles.append(xt)
@@ -122,12 +121,13 @@ def tile_consciouslm_kernel(tc, tok_emb, pos_emb, ln_w, ln_b, offs, out):
         def layer_norm(s):
             xt = xt_tiles[s]
             scales = []
-            piece_stats = x_pool.tile([P, JB * 2 * STATS], F32, name=f"stats{s}", offset=(s + 2) * X_BYTES)
             for t in range(JB):
-                for n, (first, last) in enumerate(bank_chunks(t * C, (t + 1) * C)):
-                    nc.vector.bn_stats(piece_stats[:, (2 * t + n) * STATS : (2 * t + n + 1) * STATS], xt[:, first:last])
+                chunks = bank_chunks(t * C, (t + 1) * C)
+                stats = small.tile([P, len(chunks) * STATS], F32, name="stats")
+                for n, (first, last) in enumerate(chunks):
+                    nc.vector.bn_stats(stats[:, n * STATS : (n + 1) * STATS], xt[:, first:last])
                 mean_var = small.tile([P, 2], F32, name="mean_var")
-                nc.vector.bn_aggr(mean_var[:], piece_stats[:, 2 * t * STATS : 2 * (t + 1) * STATS])
+                nc.vector.bn_aggr(mean_var[:], stats[:])
                 rstd = small.tile([P, 1], F32, name="rstd")
                 nc.scalar.activation(rstd[:], mean_var[:, 1:2], ABS_RSQRT, bias=eps[:, 0:1])
                 if s == PIECES - 1:

@@ -164,35 +164,41 @@ def tile_consciouslm_kernel(tc, tok_emb, pos_emb, ln_w, ln_b, offs, out):
                         )
 
             h_s = h_pool.tile([P, CB, PIECE], F32, name="h_s")
-            for half in range(2):
-                for t in range(JB):
-                    if s == PIECES - 1 and half == 0:
-                        h_ps = xt_psum.tile([P, BANK], F32, name="xt")
+            for b0 in range(0, CB, BANK // PIECE):
+                group = range(b0, b0 + BANK // PIECE)
+                freed_slot = s == PIECES - 1 and b0 < 2 * (BANK // PIECE)
+                if freed_slot:
+                    h_ps = xt_psum.tile([P, BANK], F32, name="xt")
+                else:
+                    h_ps = h_psum.tile([P, BANK], F32, name="h_ps")
+                for b in group:
+                    for t in range(JB):
+                        nc.tensor.transpose(
+                            h_ps[:, (b - b0) * PIECE + t * P : (b - b0) * PIECE + (t + 1) * P],
+                            xn_tiles[t][:, b * P : (b + 1) * P],
+                            ident[:],
+                        )
+                for b in group:
+                    if freed_slot:
+                        nc.vector.tensor_scalar(
+                            h_s[:, b, :],
+                            h_ps[:, (b - b0) * PIECE : (b - b0 + 1) * PIECE],
+                            wb[:, b : b + 1],
+                            wb[:, CB + b : CB + b + 1],
+                            MULT,
+                            ADD,
+                        )
                     else:
-                        h_ps = h_psum.tile([P, BANK], F32, name="h_ps")
-                    for i in range(HALF_CB):
-                        b = half * HALF_CB + i
-                        nc.tensor.transpose(h_ps[:, i * P : (i + 1) * P], xn_tiles[t][:, b * P : (b + 1) * P], ident[:])
-                    for i in range(HALF_CB):
-                        b = half * HALF_CB + i
-                        if half == 0 or s < PIECES - 1:
-                            nc.scalar.activation(
-                                h_s[:, b, t * P : (t + 1) * P],
-                                h_ps[:, i * P : (i + 1) * P],
-                                IDENTITY,
-                                bias=wb[:, CB + b : CB + b + 1],
-                                scale=wb[:, b : b + 1],
-                            )
-                        else:
-                            nc.vector.tensor_scalar(
-                                h_s[:, b, t * P : (t + 1) * P],
-                                h_ps[:, i * P : (i + 1) * P],
-                                wb[:, b : b + 1],
-                                wb[:, CB + b : CB + b + 1],
-                                MULT,
-                                ADD,
-                            )
-                nc.sync.dma_start(h_out[:, halves[half], s * PIECE : (s + 1) * PIECE], h_s[:, halves[half], :])
+                        nc.scalar.activation(
+                            h_s[:, b, :],
+                            h_ps[:, (b - b0) * PIECE : (b - b0 + 1) * PIECE],
+                            IDENTITY,
+                            bias=wb[:, CB + b : CB + b + 1],
+                            scale=wb[:, b : b + 1],
+                        )
+                nc.sync.dma_start(
+                    h_out[:, b0 : b0 + BANK // PIECE, s * PIECE : (s + 1) * PIECE], h_s[:, b0 : b0 + BANK // PIECE, :]
+                )
 
         for s in range(PIECES + 1):
             if s < PIECES:

@@ -14,21 +14,19 @@ ABS_RSQRT = mybir.ActivationFunctionType.Abs_reciprocal_sqrt
 P = 128
 C = 768
 CB = C // P
-HALF_CB = CB // 2
 V = 256
 N = 1024
-PIECE = 256
-PIECES = N // PIECE
-JB = PIECE // P
+WIDTHS = (256, 256, 256, 128, 128)
+STARTS = (0, 256, 512, 768, 896, 1024)
+PIECES = len(WIDTHS)
+LOAD = 256
 BANK = 512
+WIDE = BANK
+NARROW = C - WIDE
+GROUP = 2
 STATS = 6
 EPS = 1e-5
-POS_RING = 2
-
-
-def bank_chunks(first, last):
-    cuts = [first] + [c for c in range(0, last, BANK) if first < c] + [last]
-    return list(zip(cuts[:-1], cuts[1:]))
+FIRST_CB = 2
 
 
 def tile_consciouslm_kernel(tc, tok_emb, pos_emb, ln_w, ln_b, offs, out):
@@ -36,49 +34,37 @@ def tile_consciouslm_kernel(tc, tok_emb, pos_emb, ln_w, ln_b, offs, out):
     pos_blocks = pos_emb.rearrange("(b p) j -> p b j", p=P)
     x_out = out[0:C, :].rearrange("(b p) j -> p b j", p=P)
     h_out = out[C : 2 * C, :].rearrange("(b p) j -> p b j", p=P)
-    halves = (slice(0, HALF_CB), slice(HALF_CB, CB))
 
     with ExitStack() as ctx:
         held = ctx.enter_context(tc.tile_pool(name="held", bufs=1))
-        pos_pool = ctx.enter_context(tc.tile_pool(name="pos_pool", bufs=POS_RING))
-        x_pool = ctx.enter_context(tc.tile_pool(name="x_pool", bufs=PIECES))
-        h_pool = ctx.enter_context(tc.tile_pool(name="h_pool", bufs=PIECES))
-        xn_pool = ctx.enter_context(tc.tile_pool(name="xn_pool", bufs=4))
+        x_pool = ctx.enter_context(tc.tile_pool(name="x_pool", bufs=1))
+        xn_pool = ctx.enter_context(tc.tile_pool(name="xn_pool", bufs=2))
         small = ctx.enter_context(tc.tile_pool(name="small", bufs=4))
-        xt_psum = ctx.enter_context(tc.psum_pool(name="xt_psum", bufs=2))
-        h_psum = ctx.enter_context(tc.psum_pool(name="h_psum", bufs=2))
+        turned_psum = ctx.enter_context(tc.psum_pool(name="turned_psum", bufs=4))
+        narrow_psum = ctx.enter_context(tc.psum_pool(name="narrow_psum", bufs=1))
+        h_psum = ctx.enter_context(tc.psum_pool(name="h_psum", bufs=CB // GROUP))
 
         offsets = held.tile([P, N // 16], U16, name="offsets")
         nc.sync.dma_start(offsets[:], offs)
 
-        tok = []
-        for b in range(CB):
-            tok.append(held.tile([P, V], F32, name=f"tok{b}"))
-
-        pos_tiles = []
-        for s in range(POS_RING):
-            pos_s = pos_pool.tile([P, CB, PIECE], F32, name="pos_s")
-            pos_tiles.append(pos_s)
-
-        def pos_load(s, half):
-            return (pos_tiles[s][:, halves[half], :], pos_blocks[:, halves[half], s * PIECE : (s + 1) * PIECE])
+        tok = [held.tile([P, V], F32, name=f"tok{b}") for b in range(CB)]
+        pos = [held.tile([P, CB, LOAD], F32, name=f"pos{q}") for q in range(N // LOAD)]
+        wb_rows = held.tile([2 * CB, P], F32, name="wb_rows")
 
         def tok_load(b):
             return (tok[b][:], tok_emb[b * P : (b + 1) * P, :])
 
-        wb_rows = held.tile([2 * CB, P], F32, name="wb_rows")
+        def pos_load(q, first, end):
+            return (pos[q][:, first:end, :], pos_blocks[:, first:end, q * LOAD : (q + 1) * LOAD])
 
-        first_loads = []
-        for half in range(2):
-            first_loads.append(pos_load(0, half))
-            for b in range(half * HALF_CB, (half + 1) * HALF_CB):
-                first_loads.append(tok_load(b))
-        first_loads.append((wb_rows[0:CB, :], ln_w.rearrange("(b p) o -> b (p o)", p=P)))
-        first_loads.append((wb_rows[CB : 2 * CB, :], ln_b.rearrange("(b p) o -> b (p o)", p=P)))
-        for s in range(1, POS_RING):
-            for half in range(2):
-                first_loads.append(pos_load(s, half))
-        for n, (tile_ap, dram_ap) in enumerate(first_loads):
+        loads = [pos_load(0, 0, 1), tok_load(0), pos_load(0, 1, 3), tok_load(1), tok_load(2)]
+        loads += [pos_load(0, 3, CB), tok_load(3), tok_load(4), tok_load(5)]
+        loads += [pos_load(1, 0, 3), pos_load(1, 3, CB)]
+        loads.append((wb_rows[0:CB, :], ln_w.rearrange("(b p) o -> b (p o)", p=P)))
+        loads.append((wb_rows[CB : 2 * CB, :], ln_b.rearrange("(b p) o -> b (p o)", p=P)))
+        for q in range(2, N // LOAD):
+            loads += [pos_load(q, 0, 3), pos_load(q, 3, CB)]
+        for n, (tile_ap, dram_ap) in enumerate(loads):
             queue = nc.scalar if n % 2 == 0 else nc.sync
             queue.dma_start(tile_ap, dram_ap)
 
@@ -87,125 +73,130 @@ def tile_consciouslm_kernel(tc, tok_emb, pos_emb, ln_w, ln_b, offs, out):
         eps = held.tile([P, 1], F32, name="eps")
         nc.gpsimd.memset(eps[:], EPS)
 
-        wb_ps = h_psum.tile([P, BANK], F32, name="h_ps")
-        nc.tensor.matmul(wb_ps[:, 0 : 2 * CB], wb_rows[:], ident[0 : 2 * CB, 0 : 2 * CB], start=True, stop=True)
-        wb = held.tile([P, 2 * CB], F32, name="wb")
-        nc.scalar.copy(wb[:], wb_ps[:, 0 : 2 * CB])
-
+        looked_up = [0] * PIECES
         x_tiles = []
-        xt_tiles = []
+        turned_tiles = []
 
-        def look_up_add_and_turn(s):
-            x_s = x_pool.tile([P, CB, PIECE], F32, name="x_s")
-            x_tiles.append(x_s)
-            xt = xt_psum.tile([P, JB * C], F32, name="xt")
-            xt_tiles.append(xt)
-            piece_offsets = offsets[:, s * (PIECE // 16) : (s + 1) * (PIECE // 16)]
-            for b in range(CB):
-                nc.vector.tensor_tensor(x_s[:, b, :], tok[b][:].indirect(piece_offsets), pos_tiles[s][:, b, :], ADD)
-                for t in range(JB):
-                    nc.tensor.transpose(
-                        xt[:, t * C + b * P : t * C + (b + 1) * P], x_s[:, b, t * P : (t + 1) * P], ident[:]
-                    )
+        def blocks_of(s):
+            return range(WIDTHS[s] // P)
+
+        def turned(s, t, first, end):
+            wide, narrow = turned_tiles[s][t]
+            return wide[:, first:end] if first < WIDE else narrow[:, first - WIDE : end - WIDE]
+
+        def open_piece(s):
+            width, at = WIDTHS[s], STARTS[s] * CB * 4
+            x_first = x_pool.tile([P, FIRST_CB, width], F32, name=f"x_first{s}", offset=at)
+            at += FIRST_CB * width * 4
+            x_rest = x_pool.tile([P, CB - FIRST_CB, width], F32, name=f"x_rest{s}", offset=at)
+            x_tiles.append((x_first, x_rest))
+            wide = [turned_psum.tile([P, WIDE], F32, name="turned") for t in blocks_of(s)]
+            if width == P:
+                narrow_tile = turned_psum.tile([P, NARROW], F32, name="turned")
+            else:
+                narrow_tile = narrow_psum.tile([P, 2 * NARROW], F32, name="narrow")
+            turned_tiles.append([(wide[t], narrow_tile[:, t * NARROW : (t + 1) * NARROW]) for t in blocks_of(s)])
+
+        def look_up_add_and_turn(s, end):
+            x_first, x_rest = x_tiles[s]
+            start, width = STARTS[s], WIDTHS[s]
+            piece_offsets = offsets[:, start // 16 : (start + width) // 16]
+            for b in range(looked_up[s], end):
+                x_b = x_first[:, b, :] if b < FIRST_CB else x_rest[:, b - FIRST_CB, :]
+                pos_b = pos[start // LOAD][:, b, start % LOAD : start % LOAD + width]
+                nc.vector.tensor_tensor(x_b, tok[b][:].indirect(piece_offsets), pos_b, ADD)
+                for t in blocks_of(s):
+                    nc.tensor.transpose(turned(s, t, b * P, (b + 1) * P), x_b[:, t * P : (t + 1) * P], ident[:])
+            looked_up[s] = end
 
         def store_x(s):
-            nc.sync.dma_start(x_out[:, :, s * PIECE : (s + 1) * PIECE], x_tiles[s][:])
+            x_first, x_rest = x_tiles[s]
+            nc.sync.dma_start(x_out[:, 0:FIRST_CB, STARTS[s] : STARTS[s + 1]], x_first[:])
+            nc.sync.dma_start(x_out[:, FIRST_CB:CB, STARTS[s] : STARTS[s + 1]], x_rest[:])
 
-        def load_next_pos(s):
-            pos_s = pos_pool.tile([P, CB, PIECE], F32, name="pos_s")
-            pos_tiles.append(pos_s)
-            for half in range(2):
-                tile_ap, dram_ap = pos_load(s, half)
-                nc.sync.dma_start(tile_ap, dram_ap)
+        def statistics(s):
+            if s + 1 < PIECES:
+                at = STARTS[s + 2] * CB * 4 - 32
+                stats = [x_pool.tile([P, 2 * STATS], F32, name=f"stats{s}", offset=at)]
+            else:
+                stats = [small.tile([P, 2 * STATS], F32, name="stats_last")]
+            if len(blocks_of(s)) == 2:
+                stats.append(small.tile([P, 2 * STATS], F32, name="stats"))
+            mean_var = small.tile([P, 2, 2], F32, name="mean_var")
 
-        def layer_norm(s):
-            xt = xt_tiles[s]
-            scales = []
-            for t in range(JB):
-                chunks = bank_chunks(t * C, (t + 1) * C)
-                stats = small.tile([P, len(chunks) * STATS], F32, name="stats")
-                for n, (first, last) in enumerate(chunks):
-                    nc.vector.bn_stats(stats[:, n * STATS : (n + 1) * STATS], xt[:, first:last])
-                mean_var = small.tile([P, 2], F32, name="mean_var")
-                nc.vector.bn_aggr(mean_var[:], stats[:])
-                rstd = small.tile([P, 1], F32, name="rstd")
-                nc.scalar.activation(rstd[:], mean_var[:, 1:2], ABS_RSQRT, bias=eps[:, 0:1])
-                if s == PIECES - 1:
-                    scales.append((rstd, mean_var))
-                else:
-                    neg_mean = small.tile([P, 1], F32, name="neg_mean")
-                    nc.scalar.mul(neg_mean[:], mean_var[:, 0:1], -1.0)
-                    shift = small.tile([P, 1], F32, name="shift")
-                    nc.scalar.activation(shift[:], neg_mean[:], IDENTITY, scale=rstd[:, 0:1])
-                    scales.append((rstd, shift))
+            def join(t):
+                nc.vector.bn_aggr(mean_var[:, t, :], stats[t][:])
 
-            xn_tiles = []
-            for t in range(JB):
-                rstd, shift_or_mean = scales[t]
-                xn = xn_pool.tile([P, C], F32, name="xn")
-                xn_tiles.append(xn)
-                for first, last in bank_chunks(t * C, (t + 1) * C):
+            for t in blocks_of(s):
+                nc.vector.bn_stats(stats[t][:, 0:STATS], turned(s, t, 0, WIDE))
+                if t > 0:
+                    join(t - 1)
+                nc.vector.bn_stats(stats[t][:, STATS : 2 * STATS], turned(s, t, WIDE, C))
+            if s + 1 < PIECES and len(stats) == 2:
+                look_up_add_and_turn(s + 1, FIRST_CB + 1)
+            join(len(stats) - 1)
+            return mean_var
+
+        def scale_and_shift(s, mean_var):
+            n = len(blocks_of(s))
+            rstd = small.tile([P, 2], F32, name="rstd")
+            nc.scalar.activation(rstd[:, 0:n], mean_var[:, 0:n, 1], ABS_RSQRT, bias=eps[:, 0:1])
+            if s == PIECES - 1:
+                return [(rstd[:, t : t + 1], mean_var[:, t, 0:1]) for t in blocks_of(s)]
+            neg_mean = small.tile([P, 2], F32, name="neg_mean")
+            nc.scalar.mul(neg_mean[:, 0:n], mean_var[:, 0:n, 0], -1.0)
+            shift = small.tile([P, 2], F32, name="shift")
+            for t in blocks_of(s):
+                nc.scalar.activation(shift[:, t : t + 1], neg_mean[:, t : t + 1], IDENTITY, scale=rstd[:, t : t + 1])
+            return [(rstd[:, t : t + 1], shift[:, t : t + 1]) for t in blocks_of(s)]
+
+        def normalise(s, scales):
+            xn_tiles = [xn_pool.tile([P, C], F32, name=f"xn{t}") for t in blocks_of(s)]
+            for t, (rstd, shift_or_mean) in enumerate(scales):
+                for first, end in ((0, WIDE), (WIDE, C)):
+                    xn_part = xn_tiles[t][:, first:end]
                     if s == PIECES - 1:
-                        nc.vector.tensor_scalar(
-                            xn[:, first - t * C : last - t * C],
-                            xt[:, first:last],
-                            shift_or_mean[:, 0:1],
-                            rstd[:, 0:1],
-                            SUBTRACT,
-                            MULT,
-                        )
+                        nc.vector.tensor_scalar(xn_part, turned(s, t, first, end), shift_or_mean, rstd, SUBTRACT, MULT)
                     else:
-                        nc.scalar.activation(
-                            xn[:, first - t * C : last - t * C],
-                            xt[:, first:last],
-                            IDENTITY,
-                            bias=shift_or_mean[:, 0:1],
-                            scale=rstd[:, 0:1],
-                        )
+                        nc.scalar.activation(xn_part, turned(s, t, first, end), IDENTITY, bias=shift_or_mean, scale=rstd)
+            return xn_tiles
 
-            h_s = h_pool.tile([P, CB, PIECE], F32, name="h_s")
-            for b0 in range(0, CB, BANK // PIECE):
-                group = range(b0, b0 + BANK // PIECE)
-                freed_slot = s == PIECES - 1 and b0 < 2 * (BANK // PIECE)
-                if freed_slot:
-                    h_ps = xt_psum.tile([P, BANK], F32, name="xt")
-                else:
-                    h_ps = h_psum.tile([P, BANK], F32, name="h_ps")
-                for b in group:
-                    for t in range(JB):
+        def turn_back_and_store_h(s, xn_tiles):
+            width = WIDTHS[s]
+            h_s = held.tile([P, CB, width], F32, name=f"h{s}")
+            groups = [range(b0, b0 + GROUP) for b0 in range(0, CB, GROUP)]
+            banks = [h_psum.tile([P, GROUP, width], F32, name="h_ps") for g in groups]
+            for t in blocks_of(s):
+                for g, group in enumerate(groups):
+                    for i, b in enumerate(group):
                         nc.tensor.transpose(
-                            h_ps[:, (b - b0) * PIECE + t * P : (b - b0) * PIECE + (t + 1) * P],
-                            xn_tiles[t][:, b * P : (b + 1) * P],
-                            ident[:],
+                            banks[g][:, i, t * P : (t + 1) * P], xn_tiles[t][:, b * P : (b + 1) * P], ident[:]
                         )
-                for b in group:
-                    if freed_slot:
-                        nc.vector.tensor_scalar(
-                            h_s[:, b, :],
-                            h_ps[:, (b - b0) * PIECE : (b - b0 + 1) * PIECE],
-                            wb[:, b : b + 1],
-                            wb[:, CB + b : CB + b + 1],
-                            MULT,
-                            ADD,
-                        )
+            for g, group in enumerate(groups):
+                for i, b in enumerate(group):
+                    gain, bias = wb[:, b : b + 1], wb[:, CB + b : CB + b + 1]
+                    if s == PIECES - 1 and g == 1:
+                        nc.vector.tensor_scalar(h_s[:, b, :], banks[g][:, i, :], gain, bias, MULT, ADD)
                     else:
-                        nc.scalar.activation(
-                            h_s[:, b, :],
-                            h_ps[:, (b - b0) * PIECE : (b - b0 + 1) * PIECE],
-                            IDENTITY,
-                            bias=wb[:, CB + b : CB + b + 1],
-                            scale=wb[:, b : b + 1],
-                        )
-                nc.sync.dma_start(
-                    h_out[:, b0 : b0 + BANK // PIECE, s * PIECE : (s + 1) * PIECE], h_s[:, b0 : b0 + BANK // PIECE, :]
-                )
+                        nc.scalar.activation(h_s[:, b, :], banks[g][:, i, :], IDENTITY, bias=bias, scale=gain)
+                first, end = group[0], group[-1] + 1
+                nc.sync.dma_start(h_out[:, first:end, STARTS[s] : STARTS[s + 1]], h_s[:, first:end, :])
 
-        for s in range(PIECES + 1):
-            if s < PIECES:
-                look_up_add_and_turn(s)
-            if s + POS_RING < PIECES:
-                load_next_pos(s + POS_RING)
-            if s < PIECES:
-                store_x(s)
-            if s >= 1:
-                layer_norm(s - 1)
+        open_piece(0)
+        look_up_add_and_turn(0, CB)
+        store_x(0)
+
+        wb_ps = h_psum.tile([P, 2 * CB], F32, name="h_ps")
+        nc.tensor.matmul(wb_ps[:], wb_rows[:], ident[0 : 2 * CB, 0 : 2 * CB], start=True, stop=True)
+        wb = held.tile([P, 2 * CB], F32, name="wb")
+        nc.scalar.activation(wb[:], wb_ps[:], IDENTITY)
+
+        for s in range(PIECES):
+            if s + 1 < PIECES:
+                open_piece(s + 1)
+                look_up_add_and_turn(s + 1, FIRST_CB)
+            scales = scale_and_shift(s, statistics(s))
+            if s + 1 < PIECES:
+                look_up_add_and_turn(s + 1, CB)
+                store_x(s + 1)
+            turn_back_and_store_h(s, normalise(s, scales))

@@ -9,6 +9,7 @@ ADD = mybir.AluOpType.add
 MULT = mybir.AluOpType.mult
 SUBTRACT = mybir.AluOpType.subtract
 IDENTITY = mybir.ActivationFunctionType.Identity
+SQUARE = mybir.ActivationFunctionType.Square
 ABS_RSQRT = mybir.ActivationFunctionType.Abs_reciprocal_sqrt
 
 P = 128
@@ -16,13 +17,13 @@ C = 768
 CB = C // P
 V = 256
 N = 1024
-WIDTHS = (256, 256, 256, 128, 128)
-STARTS = (0, 256, 512, 768, 896, 1024)
+WIDTHS = (128, 256, 256, 256, 128)
+STARTS = (0, 128, 384, 640, 896, 1024)
 PIECES = len(WIDTHS)
-LOAD = 256
 BANK = 512
 WIDE = BANK
 NARROW = C - WIDE
+PARTS = ((0, WIDE), (WIDE, C))
 GROUP = 2
 STATS = 6
 EPS = 1e-5
@@ -38,8 +39,9 @@ def tile_consciouslm_kernel(tc, tok_emb, pos_emb, ln_w, ln_b, offs, out):
     with ExitStack() as ctx:
         held = ctx.enter_context(tc.tile_pool(name="held", bufs=1))
         x_pool = ctx.enter_context(tc.tile_pool(name="x_pool", bufs=1))
-        xn_pool = ctx.enter_context(tc.tile_pool(name="xn_pool", bufs=2))
+        xn_pool = ctx.enter_context(tc.tile_pool(name="xn_pool", bufs=1))
         small = ctx.enter_context(tc.tile_pool(name="small", bufs=4))
+        first_pool = ctx.enter_context(tc.tile_pool(name="first_pool", bufs=1))
         turned_psum = ctx.enter_context(tc.psum_pool(name="turned_psum", bufs=4))
         narrow_psum = ctx.enter_context(tc.psum_pool(name="narrow_psum", bufs=1))
         h_psum = ctx.enter_context(tc.psum_pool(name="h_psum", bufs=CB // GROUP))
@@ -48,30 +50,34 @@ def tile_consciouslm_kernel(tc, tok_emb, pos_emb, ln_w, ln_b, offs, out):
         nc.sync.dma_start(offsets[:], offs)
 
         tok = [held.tile([P, V], F32, name=f"tok{b}") for b in range(CB)]
-        pos = [held.tile([P, CB, LOAD], F32, name=f"pos{q}") for q in range(N // LOAD)]
+        pos = [held.tile([P, CB, WIDTHS[s]], F32, name=f"pos{s}") for s in range(PIECES)]
         wb_rows = held.tile([2 * CB, P], F32, name="wb_rows")
 
         def tok_load(b):
             return (tok[b][:], tok_emb[b * P : (b + 1) * P, :])
 
-        def pos_load(q, first, end):
-            return (pos[q][:, first:end, :], pos_blocks[:, first:end, q * LOAD : (q + 1) * LOAD])
+        def pos_load(s, first, end):
+            return (pos[s][:, first:end, :], pos_blocks[:, first:end, STARTS[s] : STARTS[s + 1]])
 
-        loads = [pos_load(0, 0, 1), tok_load(0), pos_load(0, 1, 3), tok_load(1), tok_load(2)]
-        loads += [pos_load(0, 3, CB), tok_load(3), tok_load(4), tok_load(5)]
-        loads += [pos_load(1, 0, 3), pos_load(1, 3, CB)]
+        half = CB // 2
+        loads = [pos_load(0, 0, half), tok_load(0), tok_load(1), tok_load(2), tok_load(3), pos_load(0, half, CB)]
+        loads += [tok_load(5), tok_load(4), pos_load(1, 0, half), pos_load(1, half, CB)]
+        on_both_queues = len(loads)
+        loads += [pos_load(2, 0, half), pos_load(2, half, CB)]
+        loads += [pos_load(3, 0, half)]
         loads.append((wb_rows[0:CB, :], ln_w.rearrange("(b p) o -> b (p o)", p=P)))
         loads.append((wb_rows[CB : 2 * CB, :], ln_b.rearrange("(b p) o -> b (p o)", p=P)))
-        for q in range(2, N // LOAD):
-            loads += [pos_load(q, 0, 3), pos_load(q, 3, CB)]
+        loads += [pos_load(3, half, CB), pos_load(4, 0, CB)]
         for n, (tile_ap, dram_ap) in enumerate(loads):
-            queue = nc.scalar if n % 2 == 0 else nc.sync
+            queue = nc.scalar if n < on_both_queues and n % 2 == 0 else nc.sync
             queue.dma_start(tile_ap, dram_ap)
 
         ident = held.tile([P, P], F32, name="ident")
         make_identity(nc, ident[:])
         eps = held.tile([P, 1], F32, name="eps")
         nc.gpsimd.memset(eps[:], EPS)
+        table = held.tile([P, 1], F32, name="table")
+        nc.scalar.activation(table[:], eps[:], ABS_RSQRT)
 
         looked_up = [0] * PIECES
         x_tiles = []
@@ -103,8 +109,7 @@ def tile_consciouslm_kernel(tc, tok_emb, pos_emb, ln_w, ln_b, offs, out):
             piece_offsets = offsets[:, start // 16 : (start + width) // 16]
             for b in range(looked_up[s], end):
                 x_b = x_first[:, b, :] if b < FIRST_CB else x_rest[:, b - FIRST_CB, :]
-                pos_b = pos[start // LOAD][:, b, start % LOAD : start % LOAD + width]
-                nc.vector.tensor_tensor(x_b, tok[b][:].indirect(piece_offsets), pos_b, ADD)
+                nc.vector.tensor_tensor(x_b, tok[b][:].indirect(piece_offsets), pos[s][:, b, :], ADD)
                 for t in blocks_of(s):
                     nc.tensor.transpose(turned(s, t, b * P, (b + 1) * P), x_b[:, t * P : (t + 1) * P], ident[:])
             looked_up[s] = end
@@ -113,6 +118,29 @@ def tile_consciouslm_kernel(tc, tok_emb, pos_emb, ln_w, ln_b, offs, out):
             x_first, x_rest = x_tiles[s]
             nc.sync.dma_start(x_out[:, 0:FIRST_CB, STARTS[s] : STARTS[s + 1]], x_first[:])
             nc.sync.dma_start(x_out[:, FIRST_CB:CB, STARTS[s] : STARTS[s + 1]], x_rest[:])
+
+        def first_statistics_on_scalar():
+            scratch = held.tile([P, C], F32, name="scratch")
+            sums = held.tile([P, 2], F32, name="sums")
+            squares = held.tile([P, 2], F32, name="squares")
+            part = held.tile([P, 2], F32, name="part")
+            neg_mean = held.tile([P, 1], F32, name="first_neg_mean")
+            rstd = held.tile([P, 1], F32, name="first_rstd")
+            shift = first_pool.tile([P, 1], F32, name="first_shift")
+            for n, (first, end) in enumerate(PARTS):
+                xt = turned(0, 0, first, end)
+                nc.scalar.activation(scratch[:, first:end], xt, IDENTITY, accum_out=sums[:, n : n + 1])
+            nc.scalar.activation(part[:, 0:1], sums[:, 1:2], IDENTITY, scale=-1.0 / C)
+            nc.scalar.activation(neg_mean[:, 0:1], sums[:, 0:1], IDENTITY, bias=part[:, 0:1], scale=-1.0 / C)
+            for n, (first, end) in enumerate(PARTS):
+                xt = turned(0, 0, first, end)
+                nc.scalar.activation(
+                    scratch[:, first:end], xt, SQUARE, bias=neg_mean[:, 0:1], accum_out=squares[:, n : n + 1]
+                )
+            nc.scalar.activation(part[:, 1:2], squares[:, 1:2], IDENTITY, bias=eps[:, 0:1], scale=1.0 / C)
+            nc.scalar.activation(rstd[:, 0:1], squares[:, 0:1], ABS_RSQRT, bias=part[:, 1:2], scale=1.0 / C)
+            nc.scalar.activation(shift[:, 0:1], neg_mean[:, 0:1], IDENTITY, scale=rstd[:, 0:1])
+            return rstd[:, 0:1], shift[:, 0:1]
 
         def statistics(s):
             if s + 1 < PIECES:
@@ -139,29 +167,33 @@ def tile_consciouslm_kernel(tc, tok_emb, pos_emb, ln_w, ln_b, offs, out):
 
         def scale_and_shift(s, mean_var):
             n = len(blocks_of(s))
-            rstd = small.tile([P, 2], F32, name="rstd")
-            nc.scalar.activation(rstd[:, 0:n], mean_var[:, 0:n, 1], ABS_RSQRT, bias=eps[:, 0:1])
             if s == PIECES - 1:
-                return [(rstd[:, t : t + 1], mean_var[:, t, 0:1]) for t in blocks_of(s)]
-            neg_mean = small.tile([P, 2], F32, name="neg_mean")
-            nc.scalar.mul(neg_mean[:, 0:n], mean_var[:, 0:n, 0], -1.0)
-            shift = small.tile([P, 2], F32, name="shift")
-            for t in blocks_of(s):
+                rstd = small.tile([P, n], F32, name="last_rstd")
+                nc.scalar.activation(rstd[:], mean_var[:, 0:n, 1], ABS_RSQRT, bias=eps[:, 0:1])
+                return [(rstd[:, t : t + 1], mean_var[:, t, 0:1]) for t in range(n)]
+            scale = xn_pool.tile([P, 3, n], F32, name=f"scale{s}", offset=xn_offset(s - 1))
+            rstd, neg_mean, shift = [scale[:, i, :] for i in range(3)]
+            nc.scalar.activation(rstd, mean_var[:, 0:n, 1], ABS_RSQRT, bias=eps[:, 0:1])
+            nc.scalar.mul(neg_mean, mean_var[:, 0:n, 0], -1.0)
+            for t in range(n):
                 nc.scalar.activation(shift[:, t : t + 1], neg_mean[:, t : t + 1], IDENTITY, scale=rstd[:, t : t + 1])
-            return [(rstd[:, t : t + 1], shift[:, t : t + 1]) for t in blocks_of(s)]
+            return [(rstd[:, t : t + 1], shift[:, t : t + 1]) for t in range(n)]
+
+        def xn_offset(s):
+            return (s % 2) * 2 * C * 4
 
         def normalise(s, scales):
-            xn_tiles = [xn_pool.tile([P, C], F32, name=f"xn{t}") for t in blocks_of(s)]
+            xn = xn_pool.tile([P, len(blocks_of(s)), C], F32, name=f"xn{s}", offset=xn_offset(s))
             for t, (rstd, shift_or_mean) in enumerate(scales):
-                for first, end in ((0, WIDE), (WIDE, C)):
-                    xn_part = xn_tiles[t][:, first:end]
+                for first, end in PARTS:
+                    xn_part = xn[:, t, first:end]
                     if s == PIECES - 1:
                         nc.vector.tensor_scalar(xn_part, turned(s, t, first, end), shift_or_mean, rstd, SUBTRACT, MULT)
                     else:
                         nc.scalar.activation(xn_part, turned(s, t, first, end), IDENTITY, bias=shift_or_mean, scale=rstd)
-            return xn_tiles
+            return xn
 
-        def turn_back_and_store_h(s, xn_tiles):
+        def turn_back_and_store_h(s, xn):
             width = WIDTHS[s]
             h_s = held.tile([P, CB, width], F32, name=f"h{s}")
             groups = [range(b0, b0 + GROUP) for b0 in range(0, CB, GROUP)]
@@ -170,7 +202,7 @@ def tile_consciouslm_kernel(tc, tok_emb, pos_emb, ln_w, ln_b, offs, out):
                 for g, group in enumerate(groups):
                     for i, b in enumerate(group):
                         nc.tensor.transpose(
-                            banks[g][:, i, t * P : (t + 1) * P], xn_tiles[t][:, b * P : (b + 1) * P], ident[:]
+                            banks[g][:, i, t * P : (t + 1) * P], xn[:, t, b * P : (b + 1) * P], ident[:]
                         )
             for g, group in enumerate(groups):
                 for i, b in enumerate(group):
@@ -186,17 +218,22 @@ def tile_consciouslm_kernel(tc, tok_emb, pos_emb, ln_w, ln_b, offs, out):
         look_up_add_and_turn(0, CB)
         store_x(0)
 
-        wb_ps = h_psum.tile([P, 2 * CB], F32, name="h_ps")
-        nc.tensor.matmul(wb_ps[:], wb_rows[:], ident[0 : 2 * CB, 0 : 2 * CB], start=True, stop=True)
-        wb = held.tile([P, 2 * CB], F32, name="wb")
-        nc.scalar.activation(wb[:], wb_ps[:], IDENTITY)
+        def turn_gain_and_bias():
+            wb_ps = h_psum.tile([P, 2 * CB], F32, name="h_ps")
+            nc.tensor.matmul(wb_ps[:], wb_rows[:], ident[0 : 2 * CB, 0 : 2 * CB], start=True, stop=True)
+            wb = first_pool.tile([P, 2 * CB], F32, name="wb", tag="first_shift")
+            nc.scalar.activation(wb[:], wb_ps[:], IDENTITY)
+            return wb
 
         for s in range(PIECES):
             if s + 1 < PIECES:
                 open_piece(s + 1)
                 look_up_add_and_turn(s + 1, FIRST_CB)
-            scales = scale_and_shift(s, statistics(s))
+            scales = [first_statistics_on_scalar()] if s == 0 else scale_and_shift(s, statistics(s))
             if s + 1 < PIECES:
                 look_up_add_and_turn(s + 1, CB)
                 store_x(s + 1)
-            turn_back_and_store_h(s, normalise(s, scales))
+            xn = normalise(s, scales)
+            if s == 0:
+                wb = turn_gain_and_bias()
+            turn_back_and_store_h(s, xn)

@@ -27,7 +27,7 @@ PARTS = ((0, WIDE), (WIDE, C))
 GROUP = 2
 STATS = 6
 EPS = 1e-5
-FIRST_CB = 2
+FIRST_CB = 1
 
 
 def tile_consciouslm_kernel(tc, tok_emb, pos_emb, ln_w, ln_b, offs, out):
@@ -152,17 +152,11 @@ def tile_consciouslm_kernel(tc, tok_emb, pos_emb, ln_w, ln_b, offs, out):
                 stats.append(small.tile([P, 2 * STATS], F32, name="stats"))
             mean_var = small.tile([P, 2, 2], F32, name="mean_var")
 
-            def join(t):
-                nc.vector.bn_aggr(mean_var[:, t, :], stats[t][:])
-
             for t in blocks_of(s):
                 nc.vector.bn_stats(stats[t][:, 0:STATS], turned(s, t, 0, WIDE))
-                if t > 0:
-                    join(t - 1)
                 nc.vector.bn_stats(stats[t][:, STATS : 2 * STATS], turned(s, t, WIDE, C))
-            if s + 1 < PIECES and len(stats) == 2:
-                look_up_add_and_turn(s + 1, FIRST_CB + 1)
-            join(len(stats) - 1)
+            for t in blocks_of(s):
+                nc.vector.bn_aggr(mean_var[:, t, :], stats[t][:])
             return mean_var
 
         def scale_and_shift(s, mean_var):
@@ -184,8 +178,9 @@ def tile_consciouslm_kernel(tc, tok_emb, pos_emb, ln_w, ln_b, offs, out):
 
         def normalise(s, scales):
             xn = xn_pool.tile([P, len(blocks_of(s)), C], F32, name=f"xn{s}", offset=xn_offset(s))
+            cuts = PARTS if s + 1 < PIECES else [(first, first + GROUP * P) for first in range(0, C, GROUP * P)]
             for t, (rstd, shift_or_mean) in enumerate(scales):
-                for first, end in PARTS:
+                for first, end in cuts:
                     xn_part = xn[:, t, first:end]
                     if s == PIECES - 1:
                         nc.vector.tensor_scalar(xn_part, turned(s, t, first, end), shift_or_mean, rstd, SUBTRACT, MULT)
@@ -197,7 +192,13 @@ def tile_consciouslm_kernel(tc, tok_emb, pos_emb, ln_w, ln_b, offs, out):
             width = WIDTHS[s]
             h_s = held.tile([P, CB, width], F32, name=f"h{s}")
             groups = [range(b0, b0 + GROUP) for b0 in range(0, CB, GROUP)]
-            banks = [h_psum.tile([P, GROUP, width], F32, name="h_ps") for g in groups]
+            banks = []
+            for g in range(len(groups)):
+                if s == PIECES - 1 and g > 0:
+                    bank = turned_psum.tile([P, GROUP, width], F32, name="turned")
+                else:
+                    bank = h_psum.tile([P, GROUP, width], F32, name="h_ps")
+                banks.append(bank)
             for t in blocks_of(s):
                 for g, group in enumerate(groups):
                     for i, b in enumerate(group):
@@ -207,7 +208,7 @@ def tile_consciouslm_kernel(tc, tok_emb, pos_emb, ln_w, ln_b, offs, out):
             for g, group in enumerate(groups):
                 for i, b in enumerate(group):
                     gain, bias = wb[:, b : b + 1], wb[:, CB + b : CB + b + 1]
-                    if s == PIECES - 1 and g == 1:
+                    if s == PIECES - 1 and g < 2:
                         nc.vector.tensor_scalar(h_s[:, b, :], banks[g][:, i, :], gain, bias, MULT, ADD)
                     else:
                         nc.scalar.activation(h_s[:, b, :], banks[g][:, i, :], IDENTITY, bias=bias, scale=gain)

@@ -179,8 +179,8 @@ def tile_consciouslm_kernel(tc, tok_emb, pos_emb, ln_w, ln_b, offs, out):
         def normalise(s, scales):
             xn = xn_pool.tile([P, len(blocks_of(s)), C], F32, name=f"xn{s}", offset=xn_offset(s))
             cuts = PARTS if s + 1 < PIECES else [(first, first + GROUP * P) for first in range(0, C, GROUP * P)]
-            for t, (rstd, shift_or_mean) in enumerate(scales):
-                for first, end in cuts:
+            for first, end in cuts:
+                for t, (rstd, shift_or_mean) in enumerate(scales):
                     xn_part = xn[:, t, first:end]
                     if s == PIECES - 1:
                         nc.vector.tensor_scalar(xn_part, turned(s, t, first, end), shift_or_mean, rstd, SUBTRACT, MULT)
@@ -199,12 +199,13 @@ def tile_consciouslm_kernel(tc, tok_emb, pos_emb, ln_w, ln_b, offs, out):
                 else:
                     bank = h_psum.tile([P, GROUP, width], F32, name="h_ps")
                 banks.append(bank)
-            for t in blocks_of(s):
-                for g, group in enumerate(groups):
-                    for i, b in enumerate(group):
-                        nc.tensor.transpose(
-                            banks[g][:, i, t * P : (t + 1) * P], xn[:, t, b * P : (b + 1) * P], ident[:]
-                        )
+            for some_groups in (range(0, WIDE // (GROUP * P)), range(WIDE // (GROUP * P), len(groups))):
+                for t in blocks_of(s):
+                    for g in some_groups:
+                        for i, b in enumerate(groups[g]):
+                            nc.tensor.transpose(
+                                banks[g][:, i, t * P : (t + 1) * P], xn[:, t, b * P : (b + 1) * P], ident[:]
+                            )
             for g, group in enumerate(groups):
                 for i, b in enumerate(group):
                     gain, bias = wb[:, b : b + 1], wb[:, CB + b : CB + b + 1]

@@ -25,6 +25,7 @@ WIDE = BANK
 NARROW = C - WIDE
 PARTS = ((0, WIDE), (WIDE, C))
 GROUP = 2
+GROUPS = [range(b, b + GROUP) for b in range(0, CB, GROUP)]
 STATS = 6
 EPS = 1e-5
 FIRST_CB = 1
@@ -188,33 +189,35 @@ def tile_consciouslm_kernel(tc, tok_emb, pos_emb, ln_w, ln_b, offs, out):
                         nc.scalar.activation(xn_part, turned(s, t, first, end), IDENTITY, bias=shift_or_mean, scale=rstd)
             return xn
 
-        def turn_back_and_store_h(s, xn):
+        def turn_back(s, xn):
             width = WIDTHS[s]
             h_s = held.tile([P, CB, width], F32, name=f"h{s}")
-            groups = [range(b0, b0 + GROUP) for b0 in range(0, CB, GROUP)]
             banks = []
-            for g in range(len(groups)):
+            for g in range(len(GROUPS)):
                 if s == PIECES - 1 and g > 0:
                     bank = turned_psum.tile([P, GROUP, width], F32, name="turned")
                 else:
                     bank = h_psum.tile([P, GROUP, width], F32, name="h_ps")
                 banks.append(bank)
-            for some_groups in (range(0, WIDE // (GROUP * P)), range(WIDE // (GROUP * P), len(groups))):
+            for some_groups in (range(0, WIDE // (GROUP * P)), range(WIDE // (GROUP * P), len(GROUPS))):
                 for t in blocks_of(s):
                     for g in some_groups:
-                        for i, b in enumerate(groups[g]):
+                        for i, b in enumerate(GROUPS[g]):
                             nc.tensor.transpose(
                                 banks[g][:, i, t * P : (t + 1) * P], xn[:, t, b * P : (b + 1) * P], ident[:]
                             )
-            for g, group in enumerate(groups):
-                for i, b in enumerate(group):
-                    gain, bias = wb[:, b : b + 1], wb[:, CB + b : CB + b + 1]
-                    if s == PIECES - 1 and g < 2:
-                        nc.vector.tensor_scalar(h_s[:, b, :], banks[g][:, i, :], gain, bias, MULT, ADD)
-                    else:
-                        nc.scalar.activation(h_s[:, b, :], banks[g][:, i, :], IDENTITY, bias=bias, scale=gain)
-                first, end = group[0], group[-1] + 1
-                nc.sync.dma_start(h_out[:, first:end, STARTS[s] : STARTS[s + 1]], h_s[:, first:end, :])
+            return h_s, banks
+
+        def gain_bias_and_store(s, g, h_s, banks):
+            on_vector = (s, g) in ((PIECES - 2, 0), (PIECES - 1, 0), (PIECES - 1, 1))
+            for i, b in enumerate(GROUPS[g]):
+                gain, bias = wb[:, b : b + 1], wb[:, CB + b : CB + b + 1]
+                if on_vector:
+                    nc.vector.tensor_scalar(h_s[:, b, :], banks[g][:, i, :], gain, bias, MULT, ADD)
+                else:
+                    nc.scalar.activation(h_s[:, b, :], banks[g][:, i, :], IDENTITY, bias=bias, scale=gain)
+            first, end = GROUPS[g][0], GROUPS[g][-1] + 1
+            nc.sync.dma_start(h_out[:, first:end, STARTS[s] : STARTS[s + 1]], h_s[:, first:end, :])
 
         open_piece(0)
         look_up_add_and_turn(0, CB)
@@ -232,10 +235,14 @@ def tile_consciouslm_kernel(tc, tok_emb, pos_emb, ln_w, ln_b, offs, out):
                 open_piece(s + 1)
                 look_up_add_and_turn(s + 1, FIRST_CB)
             scales = [first_statistics_on_scalar()] if s == 0 else scale_and_shift(s, statistics(s))
-            if s + 1 < PIECES:
+            if s == PIECES - 1:
+                gain_bias_and_store(s - 1, 0, h_s, banks)
+            else:
                 look_up_add_and_turn(s + 1, CB)
                 store_x(s + 1)
             xn = normalise(s, scales)
             if s == 0:
                 wb = turn_gain_and_bias()
-            turn_back_and_store_h(s, xn)
+            h_s, banks = turn_back(s, xn)
+            for g in range(1 if s == PIECES - 2 else 0, len(GROUPS)):
+                gain_bias_and_store(s, g, h_s, banks)

@@ -61,8 +61,8 @@ def tile_consciouslm_kernel(tc, tok_emb, pos_emb, ln_w, ln_b, offs, out):
             return (pos[s][:, first:end, :], pos_blocks[:, first:end, STARTS[s] : STARTS[s + 1]])
 
         half = CB // 2
-        loads = [pos_load(0, 0, half), tok_load(0), tok_load(1), tok_load(2), tok_load(3), pos_load(0, half, CB)]
-        loads += [tok_load(5), tok_load(4), pos_load(1, 0, half), pos_load(1, half, CB)]
+        loads = [pos_load(0, 0, 1), tok_load(0), tok_load(1), pos_load(0, 1, half), tok_load(2), tok_load(3)]
+        loads += [pos_load(0, half, CB), tok_load(4), tok_load(5), pos_load(1, 0, 1), pos_load(1, 1, half), pos_load(1, half, CB)]
         on_both_queues = len(loads)
         loads += [pos_load(2, 0, half), pos_load(2, half, CB)]
         loads += [pos_load(3, 0, half)]

@@ -61,7 +61,7 @@ def tile_consciouslm_kernel(tc, tok_emb, pos_emb, ln_w, ln_b, offs, out):
             return (pos[s][:, first:end, :], pos_blocks[:, first:end, STARTS[s] : STARTS[s + 1]])
 
         half = CB // 2
-        loads = [pos_load(0, 0, 1), tok_load(0), tok_load(1), pos_load(0, 1, half), tok_load(2), tok_load(3)]
+        loads = [tok_load(0), pos_load(0, 0, 1), tok_load(1), pos_load(0, 1, half), tok_load(2), tok_load(3)]
         loads += [pos_load(0, half, CB), tok_load(4), tok_load(5), pos_load(1, 0, 1), pos_load(1, 1, half), pos_load(1, half, CB)]
         on_both_queues = len(loads)
         loads += [pos_load(2, 0, half), pos_load(2, half, CB)]
@@ -131,15 +131,15 @@ def tile_consciouslm_kernel(tc, tok_emb, pos_emb, ln_w, ln_b, offs, out):
             for n, (first, end) in enumerate(PARTS):
                 xt = turned(0, 0, first, end)
                 nc.scalar.activation(scratch[:, first:end], xt, IDENTITY, accum_out=sums[:, n : n + 1])
-            nc.scalar.activation(part[:, 0:1], sums[:, 1:2], IDENTITY, scale=-1.0 / C)
-            nc.scalar.activation(neg_mean[:, 0:1], sums[:, 0:1], IDENTITY, bias=part[:, 0:1], scale=-1.0 / C)
+            nc.scalar.activation(part[:, 0:1], sums[:, 0:1], IDENTITY, scale=-1.0 / C)
+            nc.scalar.activation(neg_mean[:, 0:1], sums[:, 1:2], IDENTITY, bias=part[:, 0:1], scale=-1.0 / C)
             for n, (first, end) in enumerate(PARTS):
                 xt = turned(0, 0, first, end)
                 nc.scalar.activation(
                     scratch[:, first:end], xt, SQUARE, bias=neg_mean[:, 0:1], accum_out=squares[:, n : n + 1]
                 )
-            nc.scalar.activation(part[:, 1:2], squares[:, 1:2], IDENTITY, bias=eps[:, 0:1], scale=1.0 / C)
-            nc.scalar.activation(rstd[:, 0:1], squares[:, 0:1], ABS_RSQRT, bias=part[:, 1:2], scale=1.0 / C)
+            nc.scalar.activation(part[:, 1:2], squares[:, 0:1], IDENTITY, bias=eps[:, 0:1], scale=1.0 / C)
+            nc.scalar.activation(rstd[:, 0:1], squares[:, 1:2], ABS_RSQRT, bias=part[:, 1:2], scale=1.0 / C)
             nc.scalar.activation(shift[:, 0:1], neg_mean[:, 0:1], IDENTITY, scale=rstd[:, 0:1])
             return rstd[:, 0:1], shift[:, 0:1]
 

@@ -62,13 +62,13 @@ def tile_consciouslm_kernel(tc, tok_emb, pos_emb, ln_w, ln_b, offs, out):
 
         half = CB // 2
         loads = [tok_load(0), pos_load(0, 0, 1), tok_load(1), pos_load(0, 1, half), tok_load(2), tok_load(3)]
-        loads += [pos_load(0, half, CB), tok_load(4), tok_load(5), pos_load(1, 0, 1), pos_load(1, 1, half), pos_load(1, half, CB)]
+        loads += [pos_load(0, half, CB), tok_load(4), tok_load(5), pos_load(1, 0, 1), pos_load(1, 1, half)]
+        loads += [pos_load(1, half, half + 1)]
         on_both_queues = len(loads)
-        loads += [pos_load(2, 0, half), pos_load(2, half, CB)]
-        loads += [pos_load(3, 0, half)]
+        loads += [pos_load(1, half + 1, CB), pos_load(2, 0, 1), pos_load(2, 1, half), pos_load(2, half, CB)]
         loads.append((wb_rows[0:CB, :], ln_w.rearrange("(b p) o -> b (p o)", p=P)))
         loads.append((wb_rows[CB : 2 * CB, :], ln_b.rearrange("(b p) o -> b (p o)", p=P)))
-        loads += [pos_load(3, half, CB), pos_load(4, 0, CB)]
+        loads += [pos_load(3, 0, half), pos_load(3, half, CB), pos_load(4, 0, CB)]
         for n, (tile_ap, dram_ap) in enumerate(loads):
             queue = nc.scalar if n < on_both_queues and n % 2 == 0 else nc.sync
             queue.dma_start(tile_ap, dram_ap)

from contextlib import ExitStack

import concourse.mybir as mybir
from concourse.masks import make_identity

F32 = mybir.dt.float32
U16 = mybir.dt.uint16
ADD = mybir.AluOpType.add
MULT = mybir.AluOpType.mult
SUBTRACT = mybir.AluOpType.subtract
IDENTITY = mybir.ActivationFunctionType.Identity
SQUARE = mybir.ActivationFunctionType.Square
ABS_RSQRT = mybir.ActivationFunctionType.Abs_reciprocal_sqrt

P = 128
C = 768
CB = C // P
V = 256
N = 1024
WIDTHS = (128, 256, 256, 256, 128)
STARTS = (0, 128, 384, 640, 896, 1024)
PIECES = len(WIDTHS)
BANK = 512
WIDE = BANK
NARROW = C - WIDE
PARTS = ((0, WIDE), (WIDE, C))
GROUP = 2
GROUPS = [range(b, b + GROUP) for b in range(0, CB, GROUP)]
STATS = 6
EPS = 1e-5
FIRST_CB = 1


def tile_consciouslm_kernel(tc, tok_emb, pos_emb, ln_w, ln_b, offs, out):
    nc = tc.nc
    pos_blocks = pos_emb.rearrange("(b p) j -> p b j", p=P)
    x_out = out[0:C, :].rearrange("(b p) j -> p b j", p=P)
    h_out = out[C : 2 * C, :].rearrange("(b p) j -> p b j", p=P)

    with ExitStack() as ctx:
        held = ctx.enter_context(tc.tile_pool(name="held", bufs=1))
        x_pool = ctx.enter_context(tc.tile_pool(name="x_pool", bufs=1))
        xn_pool = ctx.enter_context(tc.tile_pool(name="xn_pool", bufs=1))
        small = ctx.enter_context(tc.tile_pool(name="small", bufs=4))
        first_pool = ctx.enter_context(tc.tile_pool(name="first_pool", bufs=1))
        turned_psum = ctx.enter_context(tc.psum_pool(name="turned_psum", bufs=4))
        narrow_psum = ctx.enter_context(tc.psum_pool(name="narrow_psum", bufs=1))
        h_psum = ctx.enter_context(tc.psum_pool(name="h_psum", bufs=CB // GROUP))

        offsets = held.tile([P, N // 16], U16, name="offsets")
        nc.sync.dma_start(offsets[:], offs)

        tok = [held.tile([P, V], F32, name=f"tok{b}") for b in range(CB)]
        pos = [held.tile([P, CB, WIDTHS[s]], F32, name=f"pos{s}") for s in range(PIECES)]
        wb_rows = held.tile([2 * CB, P], F32, name="wb_rows")

        def tok_load(b):
            return (tok[b][:], tok_emb[b * P : (b + 1) * P, :])

        def pos_load(s, first, end):
            return (pos[s][:, first:end, :], pos_blocks[:, first:end, STARTS[s] : STARTS[s + 1]])

        half = CB // 2
        loads = [tok_load(0), pos_load(0, 0, 1), tok_load(1), pos_load(0, 1, half), tok_load(2), tok_load(3)]
        loads += [pos_load(0, half, CB), tok_load(4), tok_load(5), pos_load(1, 0, 1), pos_load(1, 1, half)]
        loads += [pos_load(1, half, half + 1)]
        on_both_queues = len(loads)
        loads += [pos_load(1, half + 1, CB), pos_load(2, 0, 1), pos_load(2, 1, half), pos_load(2, half, CB)]
        loads.append((wb_rows[0:CB, :], ln_w.rearrange("(b p) o -> b (p o)", p=P)))
        loads.append((wb_rows[CB : 2 * CB, :], ln_b.rearrange("(b p) o -> b (p o)", p=P)))
        loads += [pos_load(3, 0, half), pos_load(3, half, CB), pos_load(4, 0, CB)]
        for n, (tile_ap, dram_ap) in enumerate(loads):
            queue = nc.scalar if n < on_both_queues and n % 2 == 0 else nc.sync
            queue.dma_start(tile_ap, dram_ap)

        ident = held.tile([P, P], F32, name="ident")
        make_identity(nc, ident[:])
        eps = held.tile([P, 1], F32, name="eps")
        nc.gpsimd.memset(eps[:], EPS)
        table = held.tile([P, 1], F32, name="table")
        nc.scalar.activation(table[:], eps[:], ABS_RSQRT)

        looked_up = [0] * PIECES
        x_tiles = []
        turned_tiles = []

        def blocks_of(s):
            return range(WIDTHS[s] // P)

        def turned(s, t, first, end):
            wide, narrow = turned_tiles[s][t]
            return wide[:, first:end] if first < WIDE else narrow[:, first - WIDE : end - WIDE]

        def open_piece(s):
            width, at = WIDTHS[s], STARTS[s] * CB * 4
            x_first = x_pool.tile([P, FIRST_CB, width], F32, name=f"x_first{s}", offset=at)
            at += FIRST_CB * width * 4
            x_rest = x_pool.tile([P, CB - FIRST_CB, width], F32, name=f"x_rest{s}", offset=at)
            x_tiles.append((x_first, x_rest))
            wide = [turned_psum.tile([P, WIDE], F32, name="turned") for t in blocks_of(s)]
            if width == P:
                narrow_tile = turned_psum.tile([P, NARROW], F32, name="turned")
            else:
                narrow_tile = narrow_psum.tile([P, 2 * NARROW], F32, name="narrow")
            turned_tiles.append([(wide[t], narrow_tile[:, t * NARROW : (t + 1) * NARROW]) for t in blocks_of(s)])

        def look_up_add_and_turn(s, end):
            x_first, x_rest = x_tiles[s]
            start, width = STARTS[s], WIDTHS[s]
            piece_offsets = offsets[:, start // 16 : (start + width) // 16]
            for b in range(looked_up[s], end):
                x_b = x_first[:, b, :] if b < FIRST_CB else x_rest[:, b - FIRST_CB, :]
                nc.vector.tensor_tensor(x_b, tok[b][:].indirect(piece_offsets), pos[s][:, b, :], ADD)
                for t in blocks_of(s):
                    nc.tensor.transpose(turned(s, t, b * P, (b + 1) * P), x_b[:, t * P : (t + 1) * P], ident[:])
            looked_up[s] = end

        def store_x(s):
            x_first, x_rest = x_tiles[s]
            nc.sync.dma_start(x_out[:, 0:FIRST_CB, STARTS[s] : STARTS[s + 1]], x_first[:])
            nc.sync.dma_start(x_out[:, FIRST_CB:CB, STARTS[s] : STARTS[s + 1]], x_rest[:])

        def first_statistics_on_scalar():
            scratch = held.tile([P, C], F32, name="scratch")
            sums = held.tile([P, 2], F32, name="sums")
            squares = held.tile([P, 2], F32, name="squares")
            part = held.tile([P, 2], F32, name="part")
            neg_mean = held.tile([P, 1], F32, name="first_neg_mean")
            rstd = held.tile([P, 1], F32, name="first_rstd")
            shift = first_pool.tile([P, 1], F32, name="first_shift")
            for n, (first, end) in enumerate(PARTS):
                xt = turned(0, 0, first, end)
                nc.scalar.activation(scratch[:, first:end], xt, IDENTITY, accum_out=sums[:, n : n + 1])
            nc.scalar.activation(part[:, 0:1], sums[:, 0:1], IDENTITY, scale=-1.0 / C)
            nc.scalar.activation(neg_mean[:, 0:1], sums[:, 1:2], IDENTITY, bias=part[:, 0:1], scale=-1.0 / C)
            for n, (first, end) in enumerate(PARTS):
                xt = turned(0, 0, first, end)
                nc.scalar.activation(
                    scratch[:, first:end], xt, SQUARE, bias=neg_mean[:, 0:1], accum_out=squares[:, n : n + 1]
                )
            nc.scalar.activation(part[:, 1:2], squares[:, 0:1], IDENTITY, bias=eps[:, 0:1], scale=1.0 / C)
            nc.scalar.activation(rstd[:, 0:1], squares[:, 1:2], ABS_RSQRT, bias=part[:, 1:2], scale=1.0 / C)
            nc.scalar.activation(shift[:, 0:1], neg_mean[:, 0:1], IDENTITY, scale=rstd[:, 0:1])
            return rstd[:, 0:1], shift[:, 0:1]

        def statistics(s):
            if s + 1 < PIECES:
                at = STARTS[s + 2] * CB * 4 - 32
                stats = [x_pool.tile([P, 2 * STATS], F32, name=f"stats{s}", offset=at)]
            else:
                stats = [small.tile([P, 2 * STATS], F32, name="stats_last")]
            if len(blocks_of(s)) == 2:
                stats.append(small.tile([P, 2 * STATS], F32, name="stats"))
            mean_var = small.tile([P, 2, 2], F32, name="mean_var")

            for t in blocks_of(s):
                nc.vector.bn_stats(stats[t][:, 0:STATS], turned(s, t, 0, WIDE))
                nc.vector.bn_stats(stats[t][:, STATS : 2 * STATS], turned(s, t, WIDE, C))
            for t in blocks_of(s):
                nc.vector.bn_aggr(mean_var[:, t, :], stats[t][:])
            return mean_var

        def scale_and_shift(s, mean_var):
            n = len(blocks_of(s))
            if s == PIECES - 1:
                rstd = small.tile([P, n], F32, name="last_rstd")
                nc.scalar.activation(rstd[:], mean_var[:, 0:n, 1], ABS_RSQRT, bias=eps[:, 0:1])
                return [(rstd[:, t : t + 1], mean_var[:, t, 0:1]) for t in range(n)]
            scale = xn_pool.tile([P, 3, n], F32, name=f"scale{s}", offset=xn_offset(s - 1))
            rstd, neg_mean, shift = [scale[:, i, :] for i in range(3)]
            nc.scalar.activation(rstd, mean_var[:, 0:n, 1], ABS_RSQRT, bias=eps[:, 0:1])
            nc.scalar.mul(neg_mean, mean_var[:, 0:n, 0], -1.0)
            for t in range(n):
                nc.scalar.activation(shift[:, t : t + 1], neg_mean[:, t : t + 1], IDENTITY, scale=rstd[:, t : t + 1])
            return [(rstd[:, t : t + 1], shift[:, t : t + 1]) for t in range(n)]

        def xn_offset(s):
            return (s % 2) * 2 * C * 4

        def normalise(s, scales):
            xn = xn_pool.tile([P, len(blocks_of(s)), C], F32, name=f"xn{s}", offset=xn_offset(s))
            cuts = PARTS if s + 1 < PIECES else [(first, first + GROUP * P) for first in range(0, C, GROUP * P)]
            for first, end in cuts:
                for t, (rstd, shift_or_mean) in enumerate(scales):
                    xn_part = xn[:, t, first:end]
                    if s == PIECES - 1:
                        nc.vector.tensor_scalar(xn_part, turned(s, t, first, end), shift_or_mean, rstd, SUBTRACT, MULT)
                    else:
                        nc.scalar.activation(xn_part, turned(s, t, first, end), IDENTITY, bias=shift_or_mean, scale=rstd)
            return xn

        def turn_back(s, xn):
            width = WIDTHS[s]
            h_s = held.tile([P, CB, width], F32, name=f"h{s}")
            banks = []
            for g in range(len(GROUPS)):
                if s == PIECES - 1 and g > 0:
                    bank = turned_psum.tile([P, GROUP, width], F32, name="turned")
                else:
                    bank = h_psum.tile([P, GROUP, width], F32, name="h_ps")
                banks.append(bank)
            for some_groups in (range(0, WIDE // (GROUP * P)), range(WIDE // (GROUP * P), len(GROUPS))):
                for t in blocks_of(s):
                    for g in some_groups:
                        for i, b in enumerate(GROUPS[g]):
                            nc.tensor.transpose(
                                banks[g][:, i, t * P : (t + 1) * P], xn[:, t, b * P : (b + 1) * P], ident[:]
                            )
            return h_s, banks

        def gain_bias_and_store(s, g, h_s, banks):
            on_vector = (s, g) in ((PIECES - 2, 0), (PIECES - 1, 0), (PIECES - 1, 1))
            for i, b in enumerate(GROUPS[g]):
                gain, bias = wb[:, b : b + 1], wb[:, CB + b : CB + b + 1]
                if on_vector:
                    nc.vector.tensor_scalar(h_s[:, b, :], banks[g][:, i, :], gain, bias, MULT, ADD)
                else:
                    nc.scalar.activation(h_s[:, b, :], banks[g][:, i, :], IDENTITY, bias=bias, scale=gain)
            first, end = GROUPS[g][0], GROUPS[g][-1] + 1
            nc.sync.dma_start(h_out[:, first:end, STARTS[s] : STARTS[s + 1]], h_s[:, first:end, :])

        open_piece(0)
        look_up_add_and_turn(0, CB)
        store_x(0)

        def turn_gain_and_bias():
            wb_ps = h_psum.tile([P, 2 * CB], F32, name="h_ps")
            nc.tensor.matmul(wb_ps[:], wb_rows[:], ident[0 : 2 * CB, 0 : 2 * CB], start=True, stop=True)
            wb = first_pool.tile([P, 2 * CB], F32, name="wb", tag="first_shift")
            nc.scalar.activation(wb[:], wb_ps[:], IDENTITY)
            return wb

        for s in range(PIECES):
            if s + 1 < PIECES:
                open_piece(s + 1)
                look_up_add_and_turn(s + 1, FIRST_CB)
            scales = [first_statistics_on_scalar()] if s == 0 else scale_and_shift(s, statistics(s))
            if s == PIECES - 1:
                gain_bias_and_store(s - 1, 0, h_s, banks)
            else:
                look_up_add_and_turn(s + 1, CB)
                store_x(s + 1)
            xn = normalise(s, scales)
            if s == 0:
                wb = turn_gain_and_bias()
            h_s, banks = turn_back(s, xn)
            for g in range(1 if s == PIECES - 2 else 0, len(GROUPS)):
                gain_bias_and_store(s, g, h_s, banks)
